import numpy as np
import ml_dtypes


def mxq(x, axis, fmt="e4m3"):
    dtype, down = {"e4m3": (ml_dtypes.float8_e4m3fn, 7), "e5m2": (ml_dtypes.float8_e5m2, 14)}[fmt]
    v = np.moveaxis(np.asarray(x, np.float32).astype(ml_dtypes.bfloat16).astype(np.float64), axis, -1)
    blocks = v.reshape(v.shape[:-1] + (-1, 32))
    amax = np.abs(blocks).max(-1, keepdims=True)
    byte = np.maximum(np.where(amax > 0, np.frexp(amax)[1] - 1 + 127, 0) - down, 1)
    scale = np.exp2(byte - 127.0)
    codes = (blocks / scale).astype(np.float32).astype(dtype).astype(np.float64)
    return np.moveaxis((codes * scale).reshape(v.shape), -1, axis)


WIDE = False


def mx_kscale(k):
    if not WIDE:
        return np.ones(k)
    levels = np.array([10, -10, 5, -5, 0])
    a = np.random.permutation(np.resize(levels, k // 512 * 4)).reshape(k // 512, 4)
    idx = np.arange(k)
    return np.exp2(a[idx // 512, idx % 128 // 32])


BF16 = ml_dtypes.bfloat16


def bf(x):
    return np.asarray(x, np.float32).astype(BF16)


def f64(x):
    return np.asarray(x).astype(np.float64)


B, I, J, P, D = 8, 512, 512, 32, 8
EPS = 1e-5


def stdz(t):
    m = t.mean(axis=(-1, -2), keepdims=True)
    s = t.std(axis=(-1, -2), keepdims=True, ddof=1)
    return (t - m) / (s + EPS)


def flat_softmax(t):
    e = np.exp(t - t.max(axis=(-1, -2), keepdims=True))
    return e / e.sum(axis=(-1, -2), keepdims=True)


def setup_inputs():
    s = mx_kscale(I)
    return {"x": bf((np.random.standard_normal((B, I, J)) + 0.25) * s[:, None]),
            "o_xi": bf((np.random.standard_normal((D, I, P)) * 2.0 / np.sqrt(I + P) + 2.0 / I) / s[:, None]),
            "p_xi": bf(np.random.standard_normal((D, J, P)) * 2.0 / np.sqrt(J + P)),
            "rel_o_xi": bf(np.random.standard_normal((D, I, P)) * 2.0 / np.sqrt(I + P) / s[:, None])}


def reference(x, o_xi, p_xi, rel_o_xi):
    xq = mxq(f64(x), 1, "e4m3").transpose(0, 2, 1)[:, None]
    mass = flat_softmax(xq @ mxq(f64(rel_o_xi), 1, "e4m3")).sum(-2)
    t = stdz(np.tanh(xq @ mxq(f64(o_xi), 1, "e4m3")))
    u = mxq(f64(p_xi), 1, "e4m3").transpose(0, 2, 1) @ mxq(t, 2, "e4m3")
    return stdz(np.tanh(u)), mass

@@ -1,0 +1,296 @@
+from contextlib import ExitStack
+
+import concourse.mybir as mybir
+from concourse.masks import make_identity
+
+BF16 = mybir.dt.bfloat16
+F32 = mybir.dt.float32
+I32 = mybir.dt.int32
+U32 = mybir.dt.uint32
+U8 = mybir.dt.uint8
+FP8X4 = mybir.dt.float8_e4m3fn_x4
+ACT = mybir.ActivationFunctionType
+ALU = mybir.AluOpType
+AXIS = mybir.AxisListType
+
+P = 128
+PACK = 4
+BATCH = 8
+LENGTH = 512
+WIDTH = 32
+DEPTHS = 8
+QUAD = P // WIDTH
+GROUPS = DEPTHS // QUAD
+ROUND = 4
+SETS = GROUPS * ROUND
+EPS = 1e-5
+
+FLOPS = 2 * BATCH * DEPTHS * (2 * LENGTH * LENGTH * WIDTH + LENGTH * WIDTH * WIDTH)
+
+
+def quantise(nc, codes, scales, grouped):
+    nc.vector.quantize_mx(out=codes.bitcast(FP8X4), scales=scales, in_=grouped)
+
+
+def mean_and_inverse_std(nc, pool, totals, count, half):
+    sums = totals[:, 0:SETS]
+    squares = totals[:, SETS : 2 * SETS]
+    mean = pool.tile([P, SETS], F32)
+    nc.vector.tensor_scalar_mul(out=mean[:], in0=sums, scalar1=1.0 / count)
+    mean_sum = pool.tile([P, SETS], F32)
+    nc.vector.tensor_tensor(out=mean_sum[:], in0=mean[:], in1=sums, op=ALU.mult)
+    spread = pool.tile([P, SETS], F32)
+    nc.vector.tensor_tensor(out=spread[:], in0=squares, in1=mean_sum[:], op=ALU.subtract)
+    variance = pool.tile([P, SETS], F32)
+    nc.vector.tensor_scalar(
+        out=variance[:], in0=spread[:], scalar1=1.0 / (count - 1), scalar2=0.0, op0=ALU.mult, op1=ALU.max
+    )
+    std = pool.tile([P, SETS], F32)
+    nc.gpsimd.tensor_tensor(out=std[:], in0=variance[:], in1=half[:], op=ALU.pow)
+    std_eps = pool.tile([P, SETS], F32)
+    nc.vector.tensor_scalar_add(out=std_eps[:], in0=std[:], scalar1=EPS)
+    inverse = pool.tile([P, SETS], F32)
+    nc.vector.reciprocal(out=inverse[:], in_=std_eps[:])
+    return mean, inverse
+
+
+def tile_selfprojectiondev_pb_kernel(tc, x, o_xi, p_xi, rel_o_xi, out_0, out_1):
+    nc = tc.nc
+    with ExitStack() as stack:
+        const = stack.enter_context(tc.tile_pool(name="const", bufs=1))
+        x_in = stack.enter_context(tc.tile_pool(name="x_in", bufs=BATCH))
+        x_work = stack.enter_context(tc.tile_pool(name="x_work", bufs=3))
+        x_keep = stack.enter_context(tc.tile_pool(name="x_keep", bufs=BATCH))
+        h_pool = stack.enter_context(tc.tile_pool(name="h_pool", bufs=2 * SETS))
+        unread = stack.enter_context(tc.tile_pool(name="unread", bufs=4))
+        t_work = stack.enter_context(tc.tile_pool(name="t_work", bufs=4))
+        per_round = stack.enter_context(tc.tile_pool(name="per_round", bufs=2))
+        psum_first = stack.enter_context(tc.psum_pool(name="psum_first", bufs=4))
+        psum_t = stack.enter_context(tc.psum_pool(name="psum_t", bufs=2))
+        psum_small = stack.enter_context(tc.psum_pool(name="psum_small", bufs=1))
+
+        w_raw = const.tile([P, 2, DEPTHS, PACK * WIDTH], BF16)
+        nc.scalar.dma_start(out=w_raw[:, 0], in_=o_xi.rearrange("d (p j) w -> p d (j w)", j=PACK))
+        nc.scalar.dma_start(out=w_raw[:, 1], in_=rel_o_xi.rearrange("d (p j) w -> p d (j w)", j=PACK))
+        p_raw = const.tile([P, DEPTHS, PACK * WIDTH], BF16)
+        nc.scalar.dma_start(out=p_raw[:], in_=p_xi.rearrange("d (p j) w -> p d (j w)", j=PACK))
+        x_raws = []
+        for b in range(BATCH):
+            x_raw = x_in.tile([P, PACK, LENGTH], BF16)
+            nc.sync.dma_start(out=x_raw[:], in_=x[b].rearrange("(p j) c -> p j c", j=PACK))
+            x_raws.append(x_raw)
+
+        half = const.tile([P, SETS], F32)
+        nc.gpsimd.memset(half[:], 0.5)
+        warm = const.tile([P, 1], F32)
+        nc.scalar.activation(out=warm[:], in_=half[:, 0:1], func=ACT.Tanh)
+        ident_bf = const.tile([P, P], BF16)
+        make_identity(nc, ident_bf[:])
+        ident_f = const.tile([P, P], F32)
+        make_identity(nc, ident_f[:])
+        quad_ones = const.tile([P, P], F32)
+        nc.gpsimd.memset(quad_ones[:], 0.0)
+        for q in range(QUAD):
+            rows = slice(q * WIDTH, (q + 1) * WIDTH)
+            nc.gpsimd.memset(quad_ones[rows, rows], 1.0)
+        neg_max = const.tile([P, P], F32)
+        nc.vector.memset(neg_max[:], 0.0)
+        exp_sum = const.tile([P, P], F32)
+        nc.vector.memset(exp_sum[:], 0.0)
+
+        w_grouped = const.tile([P, 2, DEPTHS * WIDTH, PACK], BF16, align_bytes=64)
+        w_codes = const.tile([P, 2 * DEPTHS * WIDTH], U32, align_bytes=64)
+        w_scales = const.tile([P, 2 * DEPTHS * WIDTH], U8, align_bytes=64)
+
+        def quantise_w(source):
+            own = slice(source * DEPTHS * WIDTH, (source + 1) * DEPTHS * WIDTH)
+            nc.vector.tensor_copy(
+                out=w_grouped[:, source].rearrange("p (d w) j -> p d w j", w=WIDTH),
+                in_=w_raw[:, source].rearrange("p d (j w) -> p d w j", j=PACK),
+            )
+            quantise(nc, w_codes[:, own], w_scales[:, own], w_grouped[:, source].rearrange("p c j -> p (c j)"))
+
+        quantise_w(0)
+
+        x_codes = []
+        x_scales = []
+
+        def first_pass(operand, b):
+            own = slice(operand * P, (operand + 1) * P)
+            bank = psum_first.tile([P, LENGTH], F32, tag="first")
+            nc.tensor.matmul_mx(
+                out=bank[:],
+                lhsT=w_codes[:, own].bitcast(FP8X4),
+                lhsT_scale=w_scales[:, own],
+                rhs=x_codes[b][:].bitcast(FP8X4),
+                rhs_scale=x_scales[b][:],
+                start=True,
+                stop=True,
+            )
+            return bank
+
+        def quantise_x(b):
+            x_grouped = x_work.tile([P, LENGTH, PACK], BF16, align_bytes=64)
+            nc.vector.tensor_copy(
+                out=x_grouped[:].rearrange("p (c i) j -> p c j i", i=4),
+                in_=x_raws[b][:].rearrange("p j (c i) -> p c j i", i=4),
+            )
+            codes = x_keep.tile([P, LENGTH], U32, align_bytes=64)
+            scales = x_keep.tile([P, LENGTH], U8, align_bytes=64)
+            quantise(nc, codes[:], scales[:], x_grouped[:].rearrange("p c j -> p (c j)"))
+            x_codes.append(codes)
+            x_scales.append(scales)
+
+        def tanh_of_z(b, h_stat, h_tiles):
+            for g in range(GROUPS):
+                col = GROUPS * (b % ROUND) + g
+                z_bank = first_pass(g, b)
+                h = h_pool.tile([P, PACK, P], F32)
+                nc.scalar.activation(
+                    out=h[:],
+                    in_=z_bank[:].rearrange("m (pj t) -> m t pj", t=PACK),
+                    func=ACT.Tanh,
+                    accum_out=h_stat[:, col : col + 1],
+                )
+                h_tiles.append(h)
+                h_squared = unread.tile([P, PACK, P], BF16, tag="unread")
+                nc.scalar.activation(
+                    out=h_squared[:], in_=h[:], func=ACT.Square, accum_out=h_stat[:, SETS + col : SETS + col + 1]
+                )
+
+        def softmax_sums(b):
+            for g in range(GROUPS):
+                col = GROUPS * b + g
+                r_bank = first_pass(GROUPS + g, b)
+                nc.vector.tensor_reduce(
+                    out=neg_max[:, col : col + 1], in_=r_bank[:], axis=AXIS.X, op=ALU.max, negate=True
+                )
+                exp_r = unread.tile([P, LENGTH], BF16, tag="unread")
+                nc.scalar.activation(
+                    out=exp_r[:],
+                    in_=r_bank[:],
+                    func=ACT.Exp,
+                    bias=neg_max[:, col : col + 1],
+                    accum_out=exp_sum[:, col : col + 1],
+                )
+
+        pz_grouped = const.tile([P, DEPTHS, P, PACK], BF16, align_bytes=64)
+        nc.vector.memset(pz_grouped[:].rearrange("p d m j -> p (d m j)").bitcast(I32), 0)
+        pz_codes = const.tile([P, DEPTHS * P], U32, align_bytes=64)
+        pz_scales = const.tile([P, DEPTHS * P], U8, align_bytes=64)
+
+        def quantise_p():
+            for d in range(DEPTHS):
+                own = slice((d % QUAD) * WIDTH, (d % QUAD + 1) * WIDTH)
+                nc.scalar.copy(out=pz_grouped[:, d, own, :], in_=p_raw[:, d].rearrange("p (j w) -> p w j", j=PACK))
+            quantise(nc, pz_codes[:], pz_scales[:], pz_grouped[:].rearrange("p d m j -> p (d m j)"))
+
+        def second_contraction(rnd, h_stat, h_tiles):
+            h_totals = psum_small.tile([P, 2 * SETS], F32, tag="totals")
+            nc.tensor.matmul(out=h_totals[:], lhsT=quad_ones[:], rhs=h_stat[:], start=True, stop=True)
+            h_mean, h_inverse = mean_and_inverse_std(nc, per_round, h_totals, LENGTH * WIDTH, half)
+
+            t_grouped = per_round.tile([P, DEPTHS, ROUND, WIDTH, PACK], BF16, align_bytes=64)
+            for bi in range(ROUND):
+                transposed = psum_t.tile([P, PACK, DEPTHS * WIDTH], BF16)
+                for g in range(GROUPS):
+                    col = GROUPS * bi + g
+                    t_rows = t_work.tile([P, PACK, P], BF16)
+                    nc.vector.tensor_scalar(
+                        out=t_rows[:],
+                        in0=h_tiles[col][:],
+                        scalar1=h_mean[:, col : col + 1],
+                        scalar2=h_inverse[:, col : col + 1],
+                        op0=ALU.subtract,
+                        op1=ALU.mult,
+                    )
+                    for t in range(PACK):
+                        nc.tensor.transpose(
+                            out=transposed[:, t, g * P : (g + 1) * P], in_=t_rows[:, t, :], identity=ident_bf[:]
+                        )
+                planes = transposed[:].rearrange("p t (d w) -> p d w t", w=WIDTH)
+                if bi % 2 == 0:
+                    nc.scalar.copy(out=t_grouped[:, :, bi, :, :], in_=planes)
+                else:
+                    nc.vector.tensor_copy(out=t_grouped[:, :, bi, :, :], in_=planes)
+            t_codes = per_round.tile([P, DEPTHS * P], U32, align_bytes=64)
+            t_scales = per_round.tile([P, DEPTHS * P], U8, align_bytes=64)
+            quantise(nc, t_codes[:], t_scales[:], t_grouped[:].rearrange("p d b w t -> p (d b w t)"))
+
+            u_bank = psum_small.tile([P, GROUPS, ROUND * WIDTH], F32, tag="u")
+            for g in range(GROUPS):
+                for q in range(QUAD):
+                    own = slice((g * QUAD + q) * P, (g * QUAD + q + 1) * P)
+                    nc.tensor.matmul_mx(
+                        out=u_bank[:, g, :],
+                        lhsT=pz_codes[:, own].bitcast(FP8X4),
+                        lhsT_scale=pz_scales[:, own],
+                        rhs=t_codes[:, own].bitcast(FP8X4),
+                        rhs_scale=t_scales[:, own],
+                        start=(q == 0),
+                        stop=(q == QUAD - 1),
+                    )
+            v_both = per_round.tile([P, 2 * SETS, WIDTH], F32)
+            v = v_both[:, 0:SETS, :]
+            nc.scalar.activation(out=v, in_=u_bank[:].rearrange("m g (b w) -> m (g b) w", w=WIDTH), func=ACT.Tanh)
+            nc.scalar.activation(out=v_both[:, SETS : 2 * SETS, :], in_=v, func=ACT.Square)
+            v_stat = per_round.tile([P, 2 * SETS], F32)
+            nc.vector.tensor_reduce(out=v_stat[:], in_=v_both[:], axis=AXIS.X, op=ALU.add)
+            v_totals = psum_small.tile([P, 2 * SETS], F32, tag="totals")
+            nc.tensor.matmul(out=v_totals[:], lhsT=quad_ones[:], rhs=v_stat[:], start=True, stop=True)
+            v_mean, v_inverse = mean_and_inverse_std(nc, per_round, v_totals, WIDTH * WIDTH, half)
+            centred = per_round.tile([P, SETS, WIDTH], F32)
+            nc.vector.tensor_tensor(
+                out=centred[:], in0=v, in1=v_mean[:].unsqueeze(2).to_broadcast([P, SETS, WIDTH]), op=ALU.subtract
+            )
+            proj = per_round.tile([P, SETS, WIDTH], F32)
+            nc.vector.tensor_tensor(
+                out=proj[:], in0=centred[:], in1=v_inverse[:].unsqueeze(2).to_broadcast([P, SETS, WIDTH]), op=ALU.mult
+            )
+            for g in range(GROUPS):
+                nc.sync.dma_start(
+                    out=out_0[rnd * ROUND : (rnd + 1) * ROUND, g * QUAD : (g + 1) * QUAD].rearrange(
+                        "b d p w -> (d p) b w"
+                    ),
+                    in_=proj[:, g * ROUND : (g + 1) * ROUND, :],
+                )
+
+        for rnd in range(BATCH // ROUND):
+            h_stat = per_round.tile([P, 2 * SETS], F32)
+            h_tiles = []
+            for b in range(rnd * ROUND, (rnd + 1) * ROUND):
+                quantise_x(b)
+                tanh_of_z(b, h_stat, h_tiles)
+            if rnd == 0:
+                quantise_p()
+            second_contraction(rnd, h_stat, h_tiles)
+        quantise_w(1)
+        for b in range(BATCH):
+            softmax_sums(b)
+
+        rows = BATCH * GROUPS
+        turned = psum_first.tile([P, 2, P], F32, tag="first")
+        nc.tensor.transpose(out=turned[:, 0, :], in_=neg_max[:], identity=ident_f[:])
+        nc.tensor.transpose(out=turned[:, 1, :], in_=exp_sum[:], identity=ident_f[:])
+        neg_max_t = turned[0:rows, 0, :].rearrange("r (d w) -> r d w", w=WIDTH)
+        exp_sum_t = turned[0:rows, 1, :].rearrange("r (d w) -> r d w", w=WIDTH)
+        shape = [rows, QUAD, WIDTH]
+        neg_top = const.tile([rows, QUAD], F32)
+        nc.vector.tensor_reduce(out=neg_top[:], in_=neg_max_t, axis=AXIS.X, op=ALU.min)
+        below_top = const.tile(shape, F32)
+        nc.vector.tensor_tensor(
+            out=below_top[:], in0=neg_top[:].unsqueeze(2).to_broadcast(shape), in1=neg_max_t, op=ALU.subtract
+        )
+        weight = const.tile(shape, F32)
+        nc.scalar.activation(out=weight[:], in_=below_top[:], func=ACT.Exp)
+        share = const.tile(shape, F32)
+        nc.vector.tensor_tensor(out=share[:], in0=weight[:], in1=exp_sum_t, op=ALU.mult)
+        whole = const.tile([rows, QUAD], F32)
+        nc.vector.tensor_reduce(out=whole[:], in_=share[:], axis=AXIS.X, op=ALU.add)
+        whole_inverse = const.tile([rows, QUAD], F32)
+        nc.vector.reciprocal(out=whole_inverse[:], in_=whole[:])
+        mass = const.tile(shape, F32)
+        nc.vector.tensor_tensor(
+            out=mass[:], in0=share[:], in1=whole_inverse[:].unsqueeze(2).to_broadcast(shape), op=ALU.mult
+        )
+        nc.sync.dma_start(out=out_1.rearrange("b (g d) w -> (b g) d w", g=GROUPS), in_=mass[:])

@@ -23,6 +23,7 @@ QUAD = P // WIDTH
 GROUPS = DEPTHS // QUAD
 ROUND = 4
 SETS = GROUPS * ROUND
+PAIR = 2
 EPS = 1e-5
 
 FLOPS = 2 * BATCH * DEPTHS * (2 * LENGTH * LENGTH * WIDTH + LENGTH * WIDTH * WIDTH)
@@ -32,24 +33,24 @@ def quantise(nc, codes, scales, grouped):
     nc.vector.quantize_mx(out=codes.bitcast(FP8X4), scales=scales, in_=grouped)
 
 
-def mean_and_inverse_std(nc, pool, totals, count, half):
-    sums = totals[:, 0:SETS]
-    squares = totals[:, SETS : 2 * SETS]
-    mean = pool.tile([P, SETS], F32)
+def mean_and_inverse_std(nc, pool, totals, sets, count, half):
+    sums = totals[:, 0:sets]
+    squares = totals[:, sets : 2 * sets]
+    mean = pool.tile([P, sets], F32, tag="mean")
     nc.vector.tensor_scalar_mul(out=mean[:], in0=sums, scalar1=1.0 / count)
-    mean_sum = pool.tile([P, SETS], F32)
+    mean_sum = pool.tile([P, sets], F32, tag="mean_sum")
     nc.vector.tensor_tensor(out=mean_sum[:], in0=mean[:], in1=sums, op=ALU.mult)
-    spread = pool.tile([P, SETS], F32)
+    spread = pool.tile([P, sets], F32, tag="spread")
     nc.vector.tensor_tensor(out=spread[:], in0=squares, in1=mean_sum[:], op=ALU.subtract)
-    variance = pool.tile([P, SETS], F32)
+    variance = pool.tile([P, sets], F32, tag="variance")
     nc.vector.tensor_scalar(
         out=variance[:], in0=spread[:], scalar1=1.0 / (count - 1), scalar2=0.0, op0=ALU.mult, op1=ALU.max
     )
-    std = pool.tile([P, SETS], F32)
-    nc.gpsimd.tensor_tensor(out=std[:], in0=variance[:], in1=half[:], op=ALU.pow)
-    std_eps = pool.tile([P, SETS], F32)
+    std = pool.tile([P, sets], F32, tag="std")
+    nc.gpsimd.tensor_tensor(out=std[:], in0=variance[:], in1=half[:, 0:sets], op=ALU.pow)
+    std_eps = pool.tile([P, sets], F32, tag="std_eps")
     nc.vector.tensor_scalar_add(out=std_eps[:], in0=std[:], scalar1=EPS)
-    inverse = pool.tile([P, SETS], F32)
+    inverse = pool.tile([P, sets], F32, tag="inverse")
     nc.vector.reciprocal(out=inverse[:], in_=std_eps[:])
     return mean, inverse
 
@@ -65,6 +66,7 @@ def tile_selfprojectiondev_pb_kernel(tc, x, o_xi, p_xi, rel_o_xi, out_0, out_1):
         unread = stack.enter_context(tc.tile_pool(name="unread", bufs=4))
         t_work = stack.enter_context(tc.tile_pool(name="t_work", bufs=4))
         per_round = stack.enter_context(tc.tile_pool(name="per_round", bufs=2))
+        stats = stack.enter_context(tc.tile_pool(name="stats", bufs=BATCH // PAIR + BATCH // ROUND))
         psum_first = stack.enter_context(tc.psum_pool(name="psum_first", bufs=4))
         psum_t = stack.enter_context(tc.psum_pool(name="psum_t", bufs=2))
         psum_small = stack.enter_context(tc.psum_pool(name="psum_small", bufs=1))
@@ -114,6 +116,9 @@ def tile_selfprojectiondev_pb_kernel(tc, x, o_xi, p_xi, rel_o_xi, out_0, out_1):
 
         x_codes = []
         x_scales = []
+        h_tiles = []
+        h_means = []
+        h_inverses = []
 
         def first_pass(operand, b):
             own = slice(operand * P, (operand + 1) * P)
@@ -141,9 +146,9 @@ def tile_selfprojectiondev_pb_kernel(tc, x, o_xi, p_xi, rel_o_xi, out_0, out_1):
             x_codes.append(codes)
             x_scales.append(scales)
 
-        def tanh_of_z(b, h_stat, h_tiles):
+        def tanh_of_z(b, h_stat):
             for g in range(GROUPS):
-                col = GROUPS * (b % ROUND) + g
+                col = GROUPS * (b % PAIR) + g
                 z_bank = first_pass(g, b)
                 h = h_pool.tile([P, PACK, P], F32)
                 nc.scalar.activation(
@@ -155,7 +160,7 @@ def tile_selfprojectiondev_pb_kernel(tc, x, o_xi, p_xi, rel_o_xi, out_0, out_1):
                 h_tiles.append(h)
                 h_squared = unread.tile([P, PACK, P], BF16, tag="unread")
                 nc.scalar.activation(
-                    out=h_squared[:], in_=h[:], func=ACT.Square, accum_out=h_stat[:, SETS + col : SETS + col + 1]
+                    out=h_squared[:], in_=h[:], func=ACT.Square, accum_out=h_stat[:, GROUPS * PAIR + col : GROUPS * PAIR + col + 1]
                 )
 
         def softmax_sums(b):
@@ -185,22 +190,26 @@ def tile_selfprojectiondev_pb_kernel(tc, x, o_xi, p_xi, rel_o_xi, out_0, out_1):
                 nc.scalar.copy(out=pz_grouped[:, d, own, :], in_=p_raw[:, d].rearrange("p (j w) -> p w j", j=PACK))
             quantise(nc, pz_codes[:], pz_scales[:], pz_grouped[:].rearrange("p d m j -> p (d m j)"))
 
-        def second_contraction(rnd, h_stat, h_tiles):
-            h_totals = psum_small.tile([P, 2 * SETS], F32, tag="totals")
+        def statistics_of_h(h_stat):
+            h_totals = psum_small.tile([P, 2 * GROUPS * PAIR], F32, tag="totals")
             nc.tensor.matmul(out=h_totals[:], lhsT=quad_ones[:], rhs=h_stat[:], start=True, stop=True)
-            h_mean, h_inverse = mean_and_inverse_std(nc, per_round, h_totals, LENGTH * WIDTH, half)
+            h_mean, h_inverse = mean_and_inverse_std(nc, stats, h_totals, GROUPS * PAIR, LENGTH * WIDTH, half)
+            h_means.append(h_mean)
+            h_inverses.append(h_inverse)
 
+        def second_contraction(rnd):
             t_grouped = per_round.tile([P, DEPTHS, ROUND, WIDTH, PACK], BF16, align_bytes=64)
             for bi in range(ROUND):
                 transposed = psum_t.tile([P, PACK, DEPTHS * WIDTH], BF16)
+                b = rnd * ROUND + bi
                 for g in range(GROUPS):
-                    col = GROUPS * bi + g
+                    col = GROUPS * (b % PAIR) + g
                     t_rows = t_work.tile([P, PACK, P], BF16)
                     nc.vector.tensor_scalar(
                         out=t_rows[:],
-                        in0=h_tiles[col][:],
-                        scalar1=h_mean[:, col : col + 1],
-                        scalar2=h_inverse[:, col : col + 1],
+                        in0=h_tiles[GROUPS * b + g][:],
+                        scalar1=h_means[b // PAIR][:, col : col + 1],
+                        scalar2=h_inverses[b // PAIR][:, col : col + 1],
                         op0=ALU.subtract,
                         op1=ALU.mult,
                     )
@@ -238,7 +247,7 @@ def tile_selfprojectiondev_pb_kernel(tc, x, o_xi, p_xi, rel_o_xi, out_0, out_1):
             nc.vector.tensor_reduce(out=v_stat[:], in_=v_both[:], axis=AXIS.X, op=ALU.add)
             v_totals = psum_small.tile([P, 2 * SETS], F32, tag="totals")
             nc.tensor.matmul(out=v_totals[:], lhsT=quad_ones[:], rhs=v_stat[:], start=True, stop=True)
-            v_mean, v_inverse = mean_and_inverse_std(nc, per_round, v_totals, WIDTH * WIDTH, half)
+            v_mean, v_inverse = mean_and_inverse_std(nc, stats, v_totals, SETS, WIDTH * WIDTH, half)
             centred = per_round.tile([P, SETS, WIDTH], F32)
             nc.vector.tensor_tensor(
                 out=centred[:], in0=v, in1=v_mean[:].unsqueeze(2).to_broadcast([P, SETS, WIDTH]), op=ALU.subtract
@@ -255,15 +264,15 @@ def tile_selfprojectiondev_pb_kernel(tc, x, o_xi, p_xi, rel_o_xi, out_0, out_1):
                     in_=proj[:, g * ROUND : (g + 1) * ROUND, :],
                 )
 
-        for rnd in range(BATCH // ROUND):
-            h_stat = per_round.tile([P, 2 * SETS], F32)
-            h_tiles = []
-            for b in range(rnd * ROUND, (rnd + 1) * ROUND):
+        for pair in range(BATCH // PAIR):
+            h_stat = stats.tile([P, 2 * GROUPS * PAIR], F32)
+            for b in range(pair * PAIR, (pair + 1) * PAIR):
                 quantise_x(b)
-                tanh_of_z(b, h_stat, h_tiles)
-            if rnd == 0:
-                quantise_p()
-            second_contraction(rnd, h_stat, h_tiles)
+                tanh_of_z(b, h_stat)
+            statistics_of_h(h_stat)
+        quantise_p()
+        for rnd in range(BATCH // ROUND):
+            second_contraction(rnd)
         quantise_w(1)
         for b in range(BATCH):
             softmax_sums(b)

@@ -25,6 +25,7 @@ ROUND = 4
 SETS = GROUPS * ROUND
 PAIR = 2
 EPS = 1e-5
+SPAN = QUAD * (P + WIDTH)
 
 FLOPS = 2 * BATCH * DEPTHS * (2 * LENGTH * LENGTH * WIDTH + LENGTH * WIDTH * WIDTH)
 
@@ -33,26 +34,48 @@ def quantise(nc, codes, scales, grouped):
     nc.vector.quantize_mx(out=codes.bitcast(FP8X4), scales=scales, in_=grouped)
 
 
-def mean_and_inverse_std(nc, pool, totals, sets, count, half):
-    sums = totals[:, 0:sets]
-    squares = totals[:, sets : 2 * sets]
-    mean = pool.tile([P, sets], F32, tag="mean")
-    nc.vector.tensor_scalar_mul(out=mean[:], in0=sums, scalar1=1.0 / count)
-    mean_sum = pool.tile([P, sets], F32, tag="mean_sum")
-    nc.vector.tensor_tensor(out=mean_sum[:], in0=mean[:], in1=sums, op=ALU.mult)
+def statistics_steps(nc, pool, totals, sets, count, half, engine):
+    both = pool.tile([P, 2 * sets], F32, tag="both")
+    mean = both[:, 0:sets]
+    mean_squared = pool.tile([P, sets], F32, tag="mean_squared")
     spread = pool.tile([P, sets], F32, tag="spread")
-    nc.vector.tensor_tensor(out=spread[:], in0=squares, in1=mean_sum[:], op=ALU.subtract)
     variance = pool.tile([P, sets], F32, tag="variance")
-    nc.vector.tensor_scalar(
-        out=variance[:], in0=spread[:], scalar1=1.0 / (count - 1), scalar2=0.0, op0=ALU.mult, op1=ALU.max
-    )
     std = pool.tile([P, sets], F32, tag="std")
-    nc.gpsimd.tensor_tensor(out=std[:], in0=variance[:], in1=half[:, 0:sets], op=ALU.pow)
     std_eps = pool.tile([P, sets], F32, tag="std_eps")
-    nc.vector.tensor_scalar_add(out=std_eps[:], in0=std[:], scalar1=EPS)
     inverse = pool.tile([P, sets], F32, tag="inverse")
-    nc.vector.reciprocal(out=inverse[:], in_=std_eps[:])
-    return mean, inverse
+
+    def read_totals():
+        nc.vector.tensor_copy(out=both[:], in_=totals[:])
+
+    def square_mean():
+        engine.tensor_tensor(out=mean_squared[:], in0=mean, in1=mean, op=ALU.mult)
+
+    def subtract():
+        engine.tensor_tensor(out=spread[:], in0=both[:, sets : 2 * sets], in1=mean_squared[:], op=ALU.subtract)
+
+    def root():
+        engine.tensor_scalar(
+            out=variance[:], in0=spread[:], scalar1=count / (count - 1), scalar2=0.0, op0=ALU.mult, op1=ALU.max
+        )
+        nc.gpsimd.tensor_tensor(out=std[:], in0=variance[:], in1=half[:, 0:sets], op=ALU.pow)
+
+    def add_eps():
+        engine.tensor_scalar(out=std_eps[:], in0=std[:], scalar1=1.0, scalar2=EPS, op0=ALU.mult, op1=ALU.add)
+
+    def invert():
+        nc.vector.reciprocal(out=inverse[:], in_=std_eps[:])
+
+    if engine is nc.gpsimd:
+        return mean, inverse, [read_totals, square_mean, subtract, root, add_eps], [invert]
+    return mean, inverse, [read_totals, square_mean, subtract, root], [add_eps, invert]
+
+
+def weave(small, large):
+    for i in range(max(len(small), len(large))):
+        if i < len(small):
+            small[i]()
+        if i < len(large):
+            large[i]()
 
 
 def tile_selfprojectiondev_pb_kernel(tc, x, o_xi, p_xi, rel_o_xi, out_0, out_1):
@@ -62,25 +85,32 @@ def tile_selfprojectiondev_pb_kernel(tc, x, o_xi, p_xi, rel_o_xi, out_0, out_1):
         x_in = stack.enter_context(tc.tile_pool(name="x_in", bufs=BATCH))
         x_work = stack.enter_context(tc.tile_pool(name="x_work", bufs=3))
         x_keep = stack.enter_context(tc.tile_pool(name="x_keep", bufs=BATCH))
-        h_pool = stack.enter_context(tc.tile_pool(name="h_pool", bufs=2 * SETS))
+        h_pool = stack.enter_context(tc.tile_pool(name="h_pool", bufs=GROUPS * BATCH))
         unread = stack.enter_context(tc.tile_pool(name="unread", bufs=4))
         t_work = stack.enter_context(tc.tile_pool(name="t_work", bufs=4))
         per_round = stack.enter_context(tc.tile_pool(name="per_round", bufs=2))
-        stats = stack.enter_context(tc.tile_pool(name="stats", bufs=BATCH // PAIR + BATCH // ROUND))
+        stats = stack.enter_context(tc.tile_pool(name="stats", bufs=6))
         psum_first = stack.enter_context(tc.psum_pool(name="psum_first", bufs=4))
         psum_t = stack.enter_context(tc.psum_pool(name="psum_t", bufs=2))
         psum_small = stack.enter_context(tc.psum_pool(name="psum_small", bufs=1))
 
         w_raw = const.tile([P, 2, DEPTHS, PACK * WIDTH], BF16)
-        nc.scalar.dma_start(out=w_raw[:, 0], in_=o_xi.rearrange("d (p j) w -> p d (j w)", j=PACK))
-        nc.scalar.dma_start(out=w_raw[:, 1], in_=rel_o_xi.rearrange("d (p j) w -> p d (j w)", j=PACK))
         p_raw = const.tile([P, DEPTHS, PACK * WIDTH], BF16)
-        nc.scalar.dma_start(out=p_raw[:], in_=p_xi.rearrange("d (p j) w -> p d (j w)", j=PACK))
         x_raws = []
-        for b in range(BATCH):
+
+        def load_x(b):
             x_raw = x_in.tile([P, PACK, LENGTH], BF16)
             nc.sync.dma_start(out=x_raw[:], in_=x[b].rearrange("(p j) c -> p j c", j=PACK))
             x_raws.append(x_raw)
+
+        nc.sync.dma_start(out=w_raw[:, 0], in_=o_xi.rearrange("d (p j) w -> p d (j w)", j=PACK))
+        load_x(0)
+        nc.sync.dma_start(out=w_raw[:, 1], in_=rel_o_xi.rearrange("d (p j) w -> p d (j w)", j=PACK))
+        load_x(1)
+        load_x(2)
+        nc.sync.dma_start(out=p_raw[:], in_=p_xi.rearrange("d (p j) w -> p d (j w)", j=PACK))
+        for b in range(3, BATCH):
+            load_x(b)
 
         half = const.tile([P, SETS], F32)
         nc.gpsimd.memset(half[:], 0.5)
@@ -90,35 +120,38 @@ def tile_selfprojectiondev_pb_kernel(tc, x, o_xi, p_xi, rel_o_xi, out_0, out_1):
         make_identity(nc, ident_bf[:])
         ident_f = const.tile([P, P], F32)
         make_identity(nc, ident_f[:])
-        quad_ones = const.tile([P, P], F32)
-        nc.gpsimd.memset(quad_ones[:], 0.0)
-        for q in range(QUAD):
-            rows = slice(q * WIDTH, (q + 1) * WIDTH)
-            nc.gpsimd.memset(quad_ones[rows, rows], 1.0)
+        quad_mean_h = const.tile([P, P], F32)
+        quad_mean_v = const.tile([P, P], F32)
+        for quad_mean, count in ((quad_mean_h, LENGTH * WIDTH), (quad_mean_v, WIDTH * WIDTH)):
+            nc.gpsimd.memset(quad_mean[:], 0.0)
+            for q in range(QUAD):
+                rows = slice(q * WIDTH, (q + 1) * WIDTH)
+                nc.gpsimd.memset(quad_mean[rows, rows], 1.0 / count)
         neg_max = const.tile([P, P], F32)
-        nc.vector.memset(neg_max[:], 0.0)
+        nc.gpsimd.memset(neg_max[:], 0.0)
         exp_sum = const.tile([P, P], F32)
-        nc.vector.memset(exp_sum[:], 0.0)
+        nc.gpsimd.memset(exp_sum[:], 0.0)
 
         w_grouped = const.tile([P, 2, DEPTHS * WIDTH, PACK], BF16, align_bytes=64)
         w_codes = const.tile([P, 2 * DEPTHS * WIDTH], U32, align_bytes=64)
         w_scales = const.tile([P, 2 * DEPTHS * WIDTH], U8, align_bytes=64)
 
+        def w_views(source):
+            return (
+                w_grouped[:, source].rearrange("p (d w) j -> p d w j", w=WIDTH),
+                w_raw[:, source].rearrange("p d (j w) -> p d w j", j=PACK),
+            )
+
         def quantise_w(source):
             own = slice(source * DEPTHS * WIDTH, (source + 1) * DEPTHS * WIDTH)
-            nc.vector.tensor_copy(
-                out=w_grouped[:, source].rearrange("p (d w) j -> p d w j", w=WIDTH),
-                in_=w_raw[:, source].rearrange("p d (j w) -> p d w j", j=PACK),
-            )
             quantise(nc, w_codes[:, own], w_scales[:, own], w_grouped[:, source].rearrange("p c j -> p (c j)"))
 
-        quantise_w(0)
-
+        x_groupeds = []
         x_codes = []
         x_scales = []
         h_tiles = []
-        h_means = []
-        h_inverses = []
+        h_means = {}
+        h_inverses = {}
 
         def first_pass(operand, b):
             own = slice(operand * P, (operand + 1) * P)
@@ -134,19 +167,27 @@ def tile_selfprojectiondev_pb_kernel(tc, x, o_xi, p_xi, rel_o_xi, out_0, out_1):
             )
             return bank
 
-        def quantise_x(b):
+        def regroup_x(b):
             x_grouped = x_work.tile([P, LENGTH, PACK], BF16, align_bytes=64)
             nc.vector.tensor_copy(
                 out=x_grouped[:].rearrange("p (c i) j -> p c j i", i=4),
                 in_=x_raws[b][:].rearrange("p j (c i) -> p c j i", i=4),
             )
+            x_groupeds.append(x_grouped)
+
+        def quantise_x(b):
             codes = x_keep.tile([P, LENGTH], U32, align_bytes=64)
             scales = x_keep.tile([P, LENGTH], U8, align_bytes=64)
-            quantise(nc, codes[:], scales[:], x_grouped[:].rearrange("p c j -> p (c j)"))
+            quantise(nc, codes[:], scales[:], x_groupeds[b][:].rearrange("p c j -> p (c j)"))
             x_codes.append(codes)
             x_scales.append(scales)
 
-        def tanh_of_z(b, h_stat):
+        h_stats = []
+
+        def tanh_of_z(b):
+            if b % PAIR == 0:
+                h_stat = stats.tile([P, 2 * GROUPS * PAIR], F32)
+                h_stats.append(h_stat)
             for g in range(GROUPS):
                 col = GROUPS * (b % PAIR) + g
                 z_bank = first_pass(g, b)
@@ -155,85 +196,133 @@ def tile_selfprojectiondev_pb_kernel(tc, x, o_xi, p_xi, rel_o_xi, out_0, out_1):
                     out=h[:],
                     in_=z_bank[:].rearrange("m (pj t) -> m t pj", t=PACK),
                     func=ACT.Tanh,
-                    accum_out=h_stat[:, col : col + 1],
+                    accum_out=h_stats[b // PAIR][:, col : col + 1],
                 )
                 h_tiles.append(h)
+            for g in range(GROUPS):
+                col = GROUPS * (PAIR + b % PAIR) + g
                 h_squared = unread.tile([P, PACK, P], BF16, tag="unread")
                 nc.scalar.activation(
-                    out=h_squared[:], in_=h[:], func=ACT.Square, accum_out=h_stat[:, GROUPS * PAIR + col : GROUPS * PAIR + col + 1]
+                    out=h_squared[:],
+                    in_=h_tiles[GROUPS * b + g][:],
+                    func=ACT.Square,
+                    accum_out=h_stats[b // PAIR][:, col : col + 1],
                 )
 
-        def softmax_sums(b):
+        from_roots = {}
+
+        def statistics_of_h(pair, engine):
+            sets = GROUPS * PAIR
+            h_totals = psum_small.tile([P, 2 * sets], F32, tag="totals")
+            nc.tensor.matmul(out=h_totals[:], lhsT=quad_mean_h[:], rhs=h_stats[pair][:], start=True, stop=True)
+            h_mean, h_inverse, to_root, from_root = statistics_steps(
+                nc, stats, h_totals, sets, LENGTH * WIDTH, half, engine
+            )
+            from_roots[pair] = from_root
+            for c in range(sets):
+                h_means[sets * pair + c] = h_mean[:, c : c + 1]
+                h_inverses[sets * pair + c] = h_inverse[:, c : c + 1]
+            return to_root
+
+        r_banks = {}
+
+        def r_of(b):
             for g in range(GROUPS):
-                col = GROUPS * b + g
                 r_bank = first_pass(GROUPS + g, b)
-                nc.vector.tensor_reduce(
-                    out=neg_max[:, col : col + 1], in_=r_bank[:], axis=AXIS.X, op=ALU.max, negate=True
-                )
-                exp_r = unread.tile([P, LENGTH], BF16, tag="unread")
-                nc.scalar.activation(
-                    out=exp_r[:],
-                    in_=r_bank[:],
-                    func=ACT.Exp,
-                    bias=neg_max[:, col : col + 1],
-                    accum_out=exp_sum[:, col : col + 1],
-                )
+                r_banks[GROUPS * b + g] = r_bank
 
-        pz_grouped = const.tile([P, DEPTHS, P, PACK], BF16, align_bytes=64)
-        nc.vector.memset(pz_grouped[:].rearrange("p d m j -> p (d m j)").bitcast(I32), 0)
-        pz_codes = const.tile([P, DEPTHS * P], U32, align_bytes=64)
-        pz_scales = const.tile([P, DEPTHS * P], U8, align_bytes=64)
+        def maximum(col):
+            nc.vector.tensor_reduce(
+                out=neg_max[:, col : col + 1], in_=r_banks[col][:], axis=AXIS.X, op=ALU.max, negate=True
+            )
+
+        def exponentials(col):
+            exp_r = unread.tile([P, LENGTH], BF16, tag="unread")
+            nc.scalar.activation(
+                out=exp_r[:],
+                in_=r_banks[col][:],
+                func=ACT.Exp,
+                bias=neg_max[:, col : col + 1],
+                accum_out=exp_sum[:, col : col + 1],
+            )
+
+        p_grouped = const.tile([P, DEPTHS * WIDTH, PACK], BF16, align_bytes=64)
+        p_codes = const.tile([P, DEPTHS * WIDTH], U32, align_bytes=64)
+        p_scales = const.tile([P, DEPTHS * WIDTH], U8, align_bytes=64)
+        pz_codes = const.tile([P, GROUPS * SPAN], U32, align_bytes=64)
+        pz_scales = const.tile([P, GROUPS * SPAN], U8, align_bytes=64)
+        nc.gpsimd.memset(pz_codes[:], 0)
+        nc.gpsimd.memset(pz_scales[:].bitcast(I32), 0)
+        nc.gpsimd.memset(p_scales[:].bitcast(I32), 0)
+
+        def regroup_p():
+            nc.vector.tensor_copy(
+                out=p_grouped[:].rearrange("p (d w) j -> p d w j", w=WIDTH),
+                in_=p_raw[:].rearrange("p d (j w) -> p d w j", j=PACK),
+            )
 
         def quantise_p():
-            for d in range(DEPTHS):
-                own = slice((d % QUAD) * WIDTH, (d % QUAD + 1) * WIDTH)
-                nc.scalar.copy(out=pz_grouped[:, d, own, :], in_=p_raw[:, d].rearrange("p (j w) -> p w j", j=PACK))
-            quantise(nc, pz_codes[:], pz_scales[:], pz_grouped[:].rearrange("p d m j -> p (d m j)"))
+            quantise(nc, p_codes[:], p_scales[:], p_grouped[:].rearrange("p c j -> p (c j)"))
 
-        def statistics_of_h(h_stat):
-            h_totals = psum_small.tile([P, 2 * GROUPS * PAIR], F32, tag="totals")
-            nc.tensor.matmul(out=h_totals[:], lhsT=quad_ones[:], rhs=h_stat[:], start=True, stop=True)
-            h_mean, h_inverse = mean_and_inverse_std(nc, stats, h_totals, GROUPS * PAIR, LENGTH * WIDTH, half)
-            h_means.append(h_mean)
-            h_inverses.append(h_inverse)
+        def place_p():
+            for source, target in ((p_codes[:].bitcast(I32), pz_codes[:].bitcast(I32)), (p_scales[:], pz_scales[:])):
+                nc.vector.tensor_copy(
+                    out=target.rearrange("p (d s) -> p d s", s=P + WIDTH)[:, :, 0:WIDTH],
+                    in_=source.rearrange("p (d w) -> p d w", w=WIDTH),
+                )
 
-        def second_contraction(rnd):
-            t_grouped = per_round.tile([P, DEPTHS, ROUND, WIDTH, PACK], BF16, align_bytes=64)
-            for bi in range(ROUND):
+        t_groupeds = {}
+
+        turned_t = {}
+
+        def t_rows_of(b, g):
+            if g == 0:
                 transposed = psum_t.tile([P, PACK, DEPTHS * WIDTH], BF16)
-                b = rnd * ROUND + bi
-                for g in range(GROUPS):
-                    col = GROUPS * (b % PAIR) + g
-                    t_rows = t_work.tile([P, PACK, P], BF16)
-                    nc.vector.tensor_scalar(
-                        out=t_rows[:],
-                        in0=h_tiles[GROUPS * b + g][:],
-                        scalar1=h_means[b // PAIR][:, col : col + 1],
-                        scalar2=h_inverses[b // PAIR][:, col : col + 1],
-                        op0=ALU.subtract,
-                        op1=ALU.mult,
-                    )
-                    for t in range(PACK):
-                        nc.tensor.transpose(
-                            out=transposed[:, t, g * P : (g + 1) * P], in_=t_rows[:, t, :], identity=ident_bf[:]
-                        )
-                planes = transposed[:].rearrange("p t (d w) -> p d w t", w=WIDTH)
-                if bi % 2 == 0:
-                    nc.scalar.copy(out=t_grouped[:, :, bi, :, :], in_=planes)
-                else:
-                    nc.vector.tensor_copy(out=t_grouped[:, :, bi, :, :], in_=planes)
+                turned_t[b] = transposed
+            t_rows = t_work.tile([P, PACK, P], BF16)
+            nc.vector.tensor_scalar(
+                out=t_rows[:],
+                in0=h_tiles[GROUPS * b + g][:],
+                scalar1=h_means[GROUPS * b + g],
+                scalar2=h_inverses[GROUPS * b + g],
+                op0=ALU.subtract,
+                op1=ALU.mult,
+            )
+            for t in range(PACK):
+                nc.tensor.transpose(
+                    out=turned_t[b][:, t, g * P : (g + 1) * P], in_=t_rows[:, t, :], identity=ident_bf[:]
+                )
+
+        def group_t(b, copy):
+            rnd, bi = divmod(b, ROUND)
+            if bi == 0:
+                t_grouped = per_round.tile([P, DEPTHS, ROUND, WIDTH, PACK], BF16, align_bytes=64)
+                t_groupeds[rnd] = t_grouped
+            copy(
+                out=t_groupeds[rnd][:, :, bi, :, :],
+                in_=turned_t[b][:].rearrange("p t (d w) -> p d w t", w=WIDTH),
+            )
+
+        v_tiles = {}
+        t_operands = {}
+
+        def quantise_t(rnd):
             t_codes = per_round.tile([P, DEPTHS * P], U32, align_bytes=64)
             t_scales = per_round.tile([P, DEPTHS * P], U8, align_bytes=64)
-            quantise(nc, t_codes[:], t_scales[:], t_grouped[:].rearrange("p d b w t -> p (d b w t)"))
+            quantise(nc, t_codes[:], t_scales[:], t_groupeds[rnd][:].rearrange("p d b w t -> p (d b w t)"))
+            t_operands[rnd] = (t_codes, t_scales)
 
+        def second_contraction(rnd):
+            t_codes, t_scales = t_operands[rnd]
             u_bank = psum_small.tile([P, GROUPS, ROUND * WIDTH], F32, tag="u")
             for g in range(GROUPS):
                 for q in range(QUAD):
                     own = slice((g * QUAD + q) * P, (g * QUAD + q + 1) * P)
+                    padded = slice(g * SPAN + q * P, g * SPAN + (q + 1) * P)
                     nc.tensor.matmul_mx(
                         out=u_bank[:, g, :],
-                        lhsT=pz_codes[:, own].bitcast(FP8X4),
-                        lhsT_scale=pz_scales[:, own],
+                        lhsT=pz_codes[:, padded].bitcast(FP8X4),
+                        lhsT_scale=pz_scales[:, padded],
                         rhs=t_codes[:, own].bitcast(FP8X4),
                         rhs_scale=t_scales[:, own],
                         start=(q == 0),
@@ -243,39 +332,160 @@ def tile_selfprojectiondev_pb_kernel(tc, x, o_xi, p_xi, rel_o_xi, out_0, out_1):
             v = v_both[:, 0:SETS, :]
             nc.scalar.activation(out=v, in_=u_bank[:].rearrange("m g (b w) -> m (g b) w", w=WIDTH), func=ACT.Tanh)
             nc.scalar.activation(out=v_both[:, SETS : 2 * SETS, :], in_=v, func=ACT.Square)
+            v_tiles[rnd] = v_both
+
+        v_parts = {}
+
+        def sums_of_v(rnd):
             v_stat = per_round.tile([P, 2 * SETS], F32)
-            nc.vector.tensor_reduce(out=v_stat[:], in_=v_both[:], axis=AXIS.X, op=ALU.add)
+            nc.vector.tensor_reduce(out=v_stat[:], in_=v_tiles[rnd][:], axis=AXIS.X, op=ALU.add)
             v_totals = psum_small.tile([P, 2 * SETS], F32, tag="totals")
-            nc.tensor.matmul(out=v_totals[:], lhsT=quad_ones[:], rhs=v_stat[:], start=True, stop=True)
-            v_mean, v_inverse = mean_and_inverse_std(nc, stats, v_totals, SETS, WIDTH * WIDTH, half)
+            nc.tensor.matmul(out=v_totals[:], lhsT=quad_mean_v[:], rhs=v_stat[:], start=True, stop=True)
+            v_parts[rnd] = v_totals
+
+        def statistics_of_v(rnd, engine):
+            v_mean, v_inverse, to_root, from_root = statistics_steps(
+                nc, stats, v_parts[rnd], SETS, WIDTH * WIDTH, half, engine
+            )
             centred = per_round.tile([P, SETS, WIDTH], F32)
-            nc.vector.tensor_tensor(
-                out=centred[:], in0=v, in1=v_mean[:].unsqueeze(2).to_broadcast([P, SETS, WIDTH]), op=ALU.subtract
-            )
             proj = per_round.tile([P, SETS, WIDTH], F32)
-            nc.vector.tensor_tensor(
-                out=proj[:], in0=centred[:], in1=v_inverse[:].unsqueeze(2).to_broadcast([P, SETS, WIDTH]), op=ALU.mult
-            )
-            for g in range(GROUPS):
-                nc.sync.dma_start(
-                    out=out_0[rnd * ROUND : (rnd + 1) * ROUND, g * QUAD : (g + 1) * QUAD].rearrange(
-                        "b d p w -> (d p) b w"
-                    ),
-                    in_=proj[:, g * ROUND : (g + 1) * ROUND, :],
+
+            def centre():
+                nc.vector.tensor_tensor(
+                    out=centred[:],
+                    in0=v_tiles[rnd][:, 0:SETS, :],
+                    in1=v_mean.unsqueeze(2).to_broadcast([P, SETS, WIDTH]),
+                    op=ALU.subtract,
                 )
 
-        for pair in range(BATCH // PAIR):
-            h_stat = stats.tile([P, 2 * GROUPS * PAIR], F32)
-            for b in range(pair * PAIR, (pair + 1) * PAIR):
-                quantise_x(b)
-                tanh_of_z(b, h_stat)
-            statistics_of_h(h_stat)
-        quantise_p()
-        for rnd in range(BATCH // ROUND):
-            second_contraction(rnd)
+            def scale():
+                nc.vector.tensor_tensor(
+                    out=proj[:],
+                    in0=centred[:],
+                    in1=v_inverse[:].unsqueeze(2).to_broadcast([P, SETS, WIDTH]),
+                    op=ALU.mult,
+                )
+                for g in range(GROUPS):
+                    nc.sync.dma_start(
+                        out=out_0[rnd * ROUND : (rnd + 1) * ROUND, g * QUAD : (g + 1) * QUAD].rearrange(
+                            "b d p w -> (d p) b w"
+                        ),
+                        in_=proj[:, g * ROUND : (g + 1) * ROUND, :],
+                    )
+
+            return to_root + [centre], from_root + [scale]
+
+        V, G, S = nc.vector, nc.gpsimd, nc.scalar
+
+        def later(function, *arguments):
+            return lambda: function(*arguments)
+
+        def rows(b):
+            return [later(t_rows_of, b, g) for g in range(GROUPS)]
+
+        def maxima(*items):
+            return [later(maximum, GROUPS * b + g) for b in items for g in range(GROUPS)]
+
+        def run(steps):
+            for step in steps:
+                step()
+
+        def both_exponentials(b):
+            for g in range(GROUPS):
+                exponentials(GROUPS * b + g)
+
+        stack.enter_context(tc.manual_schedule())
+        out, in_ = w_views(0)
+        nc.vector.tensor_copy(out=out, in_=in_)
+        quantise_w(0)
+        out, in_ = w_views(1)
+        nc.scalar.copy(out=out, in_=in_)
+        regroup_x(0)
+        quantise_x(0)
+        tanh_of_z(0)
+        regroup_x(1)
         quantise_w(1)
-        for b in range(BATCH):
-            softmax_sums(b)
+        quantise_x(1)
+        tanh_of_z(1)
+        regroup_x(2)
+        regroup_p()
+        quantise_x(2)
+        tanh_of_z(2)
+        regroup_x(3)
+        quantise_p()
+        quantise_x(3)
+        tanh_of_z(3)
+        regroup_x(4)
+        run(statistics_of_h(0, G))
+        regroup_x(5)
+        quantise_x(4)
+        tanh_of_z(4)
+        regroup_x(6)
+        quantise_x(5)
+        tanh_of_z(5)
+        place_p()
+        run(statistics_of_h(1, G))
+        run(from_roots[0])
+        regroup_x(7)
+        quantise_x(6)
+        tanh_of_z(6)
+        run(rows(0))
+        quantise_x(7)
+        tanh_of_z(7)
+        run(rows(1))
+        group_t(0, V.tensor_copy)
+        r_of(0)
+        maximum(0)
+        group_t(1, V.tensor_copy)
+        run(from_roots[1])
+        run(statistics_of_h(2, G))
+        run(rows(2) + rows(3))
+        maximum(1)
+        both_exponentials(0)
+        group_t(2, V.tensor_copy)
+        group_t(3, V.tensor_copy)
+        r_of(1)
+        maximum(2)
+        quantise_t(0)
+        second_contraction(0)
+        run(from_roots[2])
+        run(rows(4))
+        group_t(4, S.copy)
+        weave(statistics_of_h(3, V), rows(5) + maxima(1)[1:2])
+        both_exponentials(1)
+        group_t(5, S.copy)
+        r_of(2)
+        sums_of_v(0)
+        run(maxima(2))
+        both_exponentials(2)
+        r_of(3)
+        weave(from_roots[3], maxima(3)[0:1])
+        run(rows(6) + rows(7))
+        group_t(6, S.copy)
+        group_t(7, S.copy)
+        to_root, from_root = statistics_of_v(0, G)
+        run(to_root)
+        run(maxima(3)[1:2])
+        both_exponentials(3)
+        r_of(4)
+        quantise_t(1)
+        second_contraction(1)
+        run(maxima(4))
+        both_exponentials(4)
+        r_of(5)
+        run(maxima(5)[0:1])
+        sums_of_v(1)
+        run(maxima(5)[1:2])
+        both_exponentials(5)
+        r_of(6)
+        r_of(7)
+        to_root_1, from_root_1 = statistics_of_v(1, V)
+        weave(to_root_1, maxima(6))
+        both_exponentials(6)
+        run(maxima(7))
+        both_exponentials(7)
+        run(from_root)
+        run(from_root_1)
 
         rows = BATCH * GROUPS
         turned = psum_first.tile([P, 2, P], F32, tag="first")

@@ -34,7 +34,7 @@ def quantise(nc, codes, scales, grouped):
     nc.vector.quantize_mx(out=codes.bitcast(FP8X4), scales=scales, in_=grouped)
 
 
-def statistics_steps(nc, pool, totals, sets, count, half, engine):
+def statistics_steps(nc, pool, totals, sets, count, half):
     both = pool.tile([P, 2 * sets], F32, tag="both")
     mean = both[:, 0:sets]
     mean_squared = pool.tile([P, sets], F32, tag="mean_squared")
@@ -43,31 +43,35 @@ def statistics_steps(nc, pool, totals, sets, count, half, engine):
     std = pool.tile([P, sets], F32, tag="std")
     std_eps = pool.tile([P, sets], F32, tag="std_eps")
     inverse = pool.tile([P, sets], F32, tag="inverse")
+    shift = pool.tile([P, sets], F32, tag="shift")
 
     def read_totals():
         nc.vector.tensor_copy(out=both[:], in_=totals[:])
 
     def square_mean():
-        engine.tensor_tensor(out=mean_squared[:], in0=mean, in1=mean, op=ALU.mult)
+        nc.vector.tensor_tensor(out=mean_squared[:], in0=mean, in1=mean, op=ALU.mult)
 
     def subtract():
-        engine.tensor_tensor(out=spread[:], in0=both[:, sets : 2 * sets], in1=mean_squared[:], op=ALU.subtract)
+        nc.vector.tensor_tensor(out=spread[:], in0=both[:, sets : 2 * sets], in1=mean_squared[:], op=ALU.subtract)
 
     def root():
-        engine.tensor_scalar(
+        nc.vector.tensor_scalar(
             out=variance[:], in0=spread[:], scalar1=count / (count - 1), scalar2=0.0, op0=ALU.mult, op1=ALU.max
         )
         nc.gpsimd.tensor_tensor(out=std[:], in0=variance[:], in1=half[:, 0:sets], op=ALU.pow)
 
     def add_eps():
-        engine.tensor_scalar(out=std_eps[:], in0=std[:], scalar1=1.0, scalar2=EPS, op0=ALU.mult, op1=ALU.add)
+        nc.vector.tensor_scalar(out=std_eps[:], in0=std[:], scalar1=1.0, scalar2=EPS, op0=ALU.mult, op1=ALU.add)
 
     def invert():
         nc.vector.reciprocal(out=inverse[:], in_=std_eps[:])
 
-    if engine is nc.gpsimd:
-        return mean, inverse, [read_totals, square_mean, subtract, root, add_eps], [invert]
-    return mean, inverse, [read_totals, square_mean, subtract, root], [add_eps, invert]
+    def shift_step():
+        nc.vector.scalar_tensor_tensor(
+            out=shift[:], in0=mean, scalar=-1.0, in1=inverse[:], op0=ALU.mult, op1=ALU.mult
+        )
+
+    return mean, inverse, shift, [read_totals, square_mean, subtract, root], [add_eps, invert, shift_step]
 
 
 def weave(small, large):
@@ -90,8 +94,8 @@ def tile_selfprojectiondev_pb_kernel(tc, x, o_xi, p_xi, rel_o_xi, out_0, out_1):
         t_work = stack.enter_context(tc.tile_pool(name="t_work", bufs=4))
         per_round = stack.enter_context(tc.tile_pool(name="per_round", bufs=2))
         stats = stack.enter_context(tc.tile_pool(name="stats", bufs=6))
-        psum_first = stack.enter_context(tc.psum_pool(name="psum_first", bufs=4))
-        psum_t = stack.enter_context(tc.psum_pool(name="psum_t", bufs=2))
+        psum_first = stack.enter_context(tc.psum_pool(name="psum_first", bufs=2))
+        psum_t = stack.enter_context(tc.psum_pool(name="psum_t", bufs=3))
         psum_small = stack.enter_context(tc.psum_pool(name="psum_small", bufs=1))
 
         w_raw = const.tile([P, 2, DEPTHS, PACK * WIDTH], BF16)
@@ -116,21 +120,19 @@ def tile_selfprojectiondev_pb_kernel(tc, x, o_xi, p_xi, rel_o_xi, out_0, out_1):
         nc.gpsimd.memset(half[:], 0.5)
         warm = const.tile([P, 1], F32)
         nc.scalar.activation(out=warm[:], in_=half[:, 0:1], func=ACT.Tanh)
-        ident_bf = const.tile([P, P], BF16)
-        make_identity(nc, ident_bf[:])
         ident_f = const.tile([P, P], F32)
         make_identity(nc, ident_f[:])
         quad_mean_h = const.tile([P, P], F32)
         quad_mean_v = const.tile([P, P], F32)
         for quad_mean, count in ((quad_mean_h, LENGTH * WIDTH), (quad_mean_v, WIDTH * WIDTH)):
-            nc.gpsimd.memset(quad_mean[:], 0.0)
+            nc.vector.memset(quad_mean[:], 0.0)
             for q in range(QUAD):
                 rows = slice(q * WIDTH, (q + 1) * WIDTH)
-                nc.gpsimd.memset(quad_mean[rows, rows], 1.0 / count)
+                nc.vector.memset(quad_mean[rows, rows], 1.0 / count)
         neg_max = const.tile([P, P], F32)
-        nc.gpsimd.memset(neg_max[:], 0.0)
+        nc.vector.memset(neg_max[:], 0.0)
         exp_sum = const.tile([P, P], F32)
-        nc.gpsimd.memset(exp_sum[:], 0.0)
+        nc.vector.memset(exp_sum[:], 0.0)
 
         w_grouped = const.tile([P, 2, DEPTHS * WIDTH, PACK], BF16, align_bytes=64)
         w_codes = const.tile([P, 2 * DEPTHS * WIDTH], U32, align_bytes=64)
@@ -152,10 +154,11 @@ def tile_selfprojectiondev_pb_kernel(tc, x, o_xi, p_xi, rel_o_xi, out_0, out_1):
         h_tiles = []
         h_means = {}
         h_inverses = {}
+        h_shifts = {}
 
-        def first_pass(operand, b):
+        def first_pass(operand, b, tag):
             own = slice(operand * P, (operand + 1) * P)
-            bank = psum_first.tile([P, LENGTH], F32, tag="first")
+            bank = psum_first.tile([P, LENGTH], F32, tag=tag)
             nc.tensor.matmul_mx(
                 out=bank[:],
                 lhsT=w_codes[:, own].bitcast(FP8X4),
@@ -190,18 +193,18 @@ def tile_selfprojectiondev_pb_kernel(tc, x, o_xi, p_xi, rel_o_xi, out_0, out_1):
                 h_stats.append(h_stat)
             for g in range(GROUPS):
                 col = GROUPS * (b % PAIR) + g
-                z_bank = first_pass(g, b)
-                h = h_pool.tile([P, PACK, P], F32)
+                z_bank = first_pass(g, b, "z")
+                h = h_pool.tile([P, 2, P, 2], F32)
                 nc.scalar.activation(
                     out=h[:],
-                    in_=z_bank[:].rearrange("m (pj t) -> m t pj", t=PACK),
+                    in_=z_bank[:].rearrange("m (pj u e) -> m u pj e", u=2, e=2),
                     func=ACT.Tanh,
                     accum_out=h_stats[b // PAIR][:, col : col + 1],
                 )
                 h_tiles.append(h)
             for g in range(GROUPS):
                 col = GROUPS * (PAIR + b % PAIR) + g
-                h_squared = unread.tile([P, PACK, P], BF16, tag="unread")
+                h_squared = unread.tile([P, 2, P, 2], BF16, tag="unread")
                 nc.scalar.activation(
                     out=h_squared[:],
                     in_=h_tiles[GROUPS * b + g][:],
@@ -211,24 +214,25 @@ def tile_selfprojectiondev_pb_kernel(tc, x, o_xi, p_xi, rel_o_xi, out_0, out_1):
 
         from_roots = {}
 
-        def statistics_of_h(pair, engine):
+        def statistics_of_h(pair):
             sets = GROUPS * PAIR
-            h_totals = psum_small.tile([P, 2 * sets], F32, tag="totals")
+            h_totals = psum_small.tile([P, 2 * sets], F32, tag="small")
             nc.tensor.matmul(out=h_totals[:], lhsT=quad_mean_h[:], rhs=h_stats[pair][:], start=True, stop=True)
-            h_mean, h_inverse, to_root, from_root = statistics_steps(
-                nc, stats, h_totals, sets, LENGTH * WIDTH, half, engine
+            h_mean, h_inverse, h_shift, to_root, from_root = statistics_steps(
+                nc, stats, h_totals, sets, LENGTH * WIDTH, half
             )
             from_roots[pair] = from_root
             for c in range(sets):
                 h_means[sets * pair + c] = h_mean[:, c : c + 1]
                 h_inverses[sets * pair + c] = h_inverse[:, c : c + 1]
+                h_shifts[sets * pair + c] = h_shift[:, c : c + 1]
             return to_root
 
         r_banks = {}
 
         def r_of(b):
             for g in range(GROUPS):
-                r_bank = first_pass(GROUPS + g, b)
+                r_bank = first_pass(GROUPS + g, b, "r" if b % 2 == 0 else "z")
                 r_banks[GROUPS * b + g] = r_bank
 
         def maximum(col):
@@ -251,9 +255,9 @@ def tile_selfprojectiondev_pb_kernel(tc, x, o_xi, p_xi, rel_o_xi, out_0, out_1):
         p_scales = const.tile([P, DEPTHS * WIDTH], U8, align_bytes=64)
         pz_codes = const.tile([P, GROUPS * SPAN], U32, align_bytes=64)
         pz_scales = const.tile([P, GROUPS * SPAN], U8, align_bytes=64)
-        nc.gpsimd.memset(pz_codes[:], 0)
-        nc.gpsimd.memset(pz_scales[:].bitcast(I32), 0)
-        nc.gpsimd.memset(p_scales[:].bitcast(I32), 0)
+        nc.vector.memset(pz_codes[:].bitcast(I32), 0)
+        nc.vector.memset(pz_scales[:].bitcast(I32), 0)
+        nc.vector.memset(p_scales[:].bitcast(I32), 0)
 
         def regroup_p():
             nc.vector.tensor_copy(
@@ -275,33 +279,42 @@ def tile_selfprojectiondev_pb_kernel(tc, x, o_xi, p_xi, rel_o_xi, out_0, out_1):
 
         turned_t = {}
 
-        def t_rows_of(b, g):
+        def t_rows_of(b, g, on_scalar):
             if g == 0:
-                transposed = psum_t.tile([P, PACK, DEPTHS * WIDTH], BF16)
+                transposed = psum_t.tile([P, 2, DEPTHS * WIDTH], F32)
                 turned_t[b] = transposed
-            t_rows = t_work.tile([P, PACK, P], BF16)
-            nc.vector.tensor_scalar(
-                out=t_rows[:],
-                in0=h_tiles[GROUPS * b + g][:],
-                scalar1=h_means[GROUPS * b + g],
-                scalar2=h_inverses[GROUPS * b + g],
-                op0=ALU.subtract,
-                op1=ALU.mult,
-            )
-            for t in range(PACK):
+            t_rows = t_work.tile([P, 2, P, 2], BF16)
+            tile = GROUPS * b + g
+            if on_scalar:
+                nc.scalar.activation(
+                    out=t_rows[:],
+                    in_=h_tiles[tile][:],
+                    func=ACT.Identity,
+                    scale=h_inverses[tile],
+                    bias=h_shifts[tile],
+                )
+            else:
+                nc.vector.tensor_scalar(
+                    out=t_rows[:],
+                    in0=h_tiles[tile][:],
+                    scalar1=h_means[tile],
+                    scalar2=h_inverses[tile],
+                    op0=ALU.subtract,
+                    op1=ALU.mult,
+                )
+            words = t_rows[:].rearrange("m u pj e -> m (u pj e)").bitcast(F32)
+            for u in range(2):
                 nc.tensor.transpose(
-                    out=turned_t[b][:, t, g * P : (g + 1) * P], in_=t_rows[:, t, :], identity=ident_bf[:]
+                    out=turned_t[b][:, u, g * P : (g + 1) * P], in_=words[:, u * P : (u + 1) * P], identity=ident_f[:]
                 )
 
         def group_t(b, copy):
             rnd, bi = divmod(b, ROUND)
-            if bi == 0:
-                t_grouped = per_round.tile([P, DEPTHS, ROUND, WIDTH, PACK], BF16, align_bytes=64)
+            if rnd not in t_groupeds:
+                t_grouped = per_round.tile([P, DEPTHS * ROUND * WIDTH * PACK], BF16, align_bytes=64)
                 t_groupeds[rnd] = t_grouped
-            copy(
-                out=t_groupeds[rnd][:, :, bi, :, :],
-                in_=turned_t[b][:].rearrange("p t (d w) -> p d w t", w=WIDTH),
-            )
+            words = t_groupeds[rnd][:].bitcast(F32).rearrange("p (d b w u) -> p d b w u", b=ROUND, w=WIDTH, u=2)
+            copy(out=words[:, :, bi], in_=turned_t[b][:].rearrange("p u (d w) -> p d w u", w=WIDTH))
 
         v_tiles = {}
         t_operands = {}
@@ -309,12 +322,12 @@ def tile_selfprojectiondev_pb_kernel(tc, x, o_xi, p_xi, rel_o_xi, out_0, out_1):
         def quantise_t(rnd):
             t_codes = per_round.tile([P, DEPTHS * P], U32, align_bytes=64)
             t_scales = per_round.tile([P, DEPTHS * P], U8, align_bytes=64)
-            quantise(nc, t_codes[:], t_scales[:], t_groupeds[rnd][:].rearrange("p d b w t -> p (d b w t)"))
+            quantise(nc, t_codes[:], t_scales[:], t_groupeds[rnd][:])
             t_operands[rnd] = (t_codes, t_scales)
 
         def second_contraction(rnd):
             t_codes, t_scales = t_operands[rnd]
-            u_bank = psum_small.tile([P, GROUPS, ROUND * WIDTH], F32, tag="u")
+            u_bank = psum_small.tile([P, GROUPS, ROUND * WIDTH], F32, tag="small")
             for g in range(GROUPS):
                 for q in range(QUAD):
                     own = slice((g * QUAD + q) * P, (g * QUAD + q + 1) * P)
@@ -339,13 +352,13 @@ def tile_selfprojectiondev_pb_kernel(tc, x, o_xi, p_xi, rel_o_xi, out_0, out_1):
         def sums_of_v(rnd):
             v_stat = per_round.tile([P, 2 * SETS], F32)
             nc.vector.tensor_reduce(out=v_stat[:], in_=v_tiles[rnd][:], axis=AXIS.X, op=ALU.add)
-            v_totals = psum_small.tile([P, 2 * SETS], F32, tag="totals")
+            v_totals = psum_small.tile([P, 2 * SETS], F32, tag="small")
             nc.tensor.matmul(out=v_totals[:], lhsT=quad_mean_v[:], rhs=v_stat[:], start=True, stop=True)
             v_parts[rnd] = v_totals
 
-        def statistics_of_v(rnd, engine):
-            v_mean, v_inverse, to_root, from_root = statistics_steps(
-                nc, stats, v_parts[rnd], SETS, WIDTH * WIDTH, half, engine
+        def statistics_of_v(rnd):
+            v_mean, v_inverse, v_shift, to_root, from_root = statistics_steps(
+                nc, stats, v_parts[rnd], SETS, WIDTH * WIDTH, half
             )
             centred = per_round.tile([P, SETS, WIDTH], F32)
             proj = per_round.tile([P, SETS, WIDTH], F32)
@@ -373,15 +386,15 @@ def tile_selfprojectiondev_pb_kernel(tc, x, o_xi, p_xi, rel_o_xi, out_0, out_1):
                         in_=proj[:, g * ROUND : (g + 1) * ROUND, :],
                     )
 
-            return to_root + [centre], from_root + [scale]
+            return to_root + [centre], from_root[0:2] + [scale]
 
-        V, G, S = nc.vector, nc.gpsimd, nc.scalar
+        V, S = nc.vector, nc.scalar
 
         def later(function, *arguments):
             return lambda: function(*arguments)
 
-        def rows(b):
-            return [later(t_rows_of, b, g) for g in range(GROUPS)]
+        def rows(b, *on_scalar):
+            return [later(t_rows_of, b, g, on_scalar[g]) for g in range(GROUPS)]
 
         def maxima(*items):
             return [later(maximum, GROUPS * b + g) for b in items for g in range(GROUPS)]
@@ -414,85 +427,84 @@ def tile_selfprojectiondev_pb_kernel(tc, x, o_xi, p_xi, rel_o_xi, out_0, out_1):
         regroup_x(3)
         quantise_p()
         quantise_x(3)
+        to_root = statistics_of_h(0)
+        r_of(0)
         tanh_of_z(3)
-        regroup_x(4)
-        run(statistics_of_h(0, G))
-        regroup_x(5)
-        quantise_x(4)
+        weave(to_root[0:3], [later(regroup_x, 4), place_p, later(quantise_x, 4)])
         tanh_of_z(4)
+        regroup_x(5)
+        run(to_root[3:] + maxima(0))
         regroup_x(6)
         quantise_x(5)
+        to_root = statistics_of_h(1)
         tanh_of_z(5)
-        place_p()
-        run(statistics_of_h(1, G))
         run(from_roots[0])
         regroup_x(7)
+        weave(to_root[0:3], rows(0, False, False))
         quantise_x(6)
         tanh_of_z(6)
-        run(rows(0))
-        quantise_x(7)
-        tanh_of_z(7)
-        run(rows(1))
+        run(rows(1, False, False))
+        run(to_root[3:])
         group_t(0, V.tensor_copy)
-        r_of(0)
-        maximum(0)
         group_t(1, V.tensor_copy)
-        run(from_roots[1])
-        run(statistics_of_h(2, G))
-        run(rows(2) + rows(3))
-        maximum(1)
+        quantise_x(7)
+        to_root = statistics_of_h(2)
+        tanh_of_z(7)
+        weave(from_roots[1], to_root[0:3])
+        run(rows(2, False, False) + rows(3, False, False))
         both_exponentials(0)
+        run(to_root[3:])
         group_t(2, V.tensor_copy)
-        group_t(3, V.tensor_copy)
         r_of(1)
+        group_t(3, V.tensor_copy)
         maximum(2)
+        to_root = statistics_of_h(3)
+        maximum(3)
+        r_of(2)
         quantise_t(0)
         second_contraction(0)
-        run(from_roots[2])
-        run(rows(4))
-        group_t(4, S.copy)
-        weave(statistics_of_h(3, V), rows(5) + maxima(1)[1:2])
         both_exponentials(1)
-        group_t(5, S.copy)
-        r_of(2)
-        sums_of_v(0)
-        run(maxima(2))
-        both_exponentials(2)
+        weave(to_root[0:3], from_roots[2])
+        run(to_root[3:] + maxima(2))
         r_of(3)
-        weave(from_roots[3], maxima(3)[0:1])
-        run(rows(6) + rows(7))
+        run(rows(4, False, True) + rows(5, False, True))
+        both_exponentials(2)
+        group_t(4, S.copy)
+        sums_of_v(0)
+        group_t(5, S.copy)
+        weave(from_roots[3], maxima(3))
+        run(rows(6, False, True) + rows(7, False, True))
         group_t(6, S.copy)
         group_t(7, S.copy)
-        to_root, from_root = statistics_of_v(0, G)
-        run(to_root)
-        run(maxima(3)[1:2])
-        both_exponentials(3)
         r_of(4)
+        to_root, from_root = statistics_of_v(0)
+        weave(to_root[0:3], maxima(4))
+        both_exponentials(3)
+        r_of(5)
         quantise_t(1)
         second_contraction(1)
-        run(maxima(4))
         both_exponentials(4)
-        r_of(5)
-        run(maxima(5)[0:1])
-        sums_of_v(1)
-        run(maxima(5)[1:2])
-        both_exponentials(5)
+        run(to_root[3:4] + maxima(5))
         r_of(6)
+        run(maxima(6)[0:1] + to_root[4:])
+        sums_of_v(1)
+        both_exponentials(5)
         r_of(7)
-        to_root_1, from_root_1 = statistics_of_v(1, V)
-        weave(to_root_1, maxima(6))
+        run(maxima(6)[1:2])
+        to_root_1, from_root_1 = statistics_of_v(1)
+        weave(to_root_1[0:4], from_root[0:2])
         both_exponentials(6)
         run(maxima(7))
         both_exponentials(7)
-        run(from_root)
-        run(from_root_1)
+        run(from_root[2:] + to_root_1[4:] + from_root_1)
 
         rows = BATCH * GROUPS
-        turned = psum_first.tile([P, 2, P], F32, tag="first")
-        nc.tensor.transpose(out=turned[:, 0, :], in_=neg_max[:], identity=ident_f[:])
-        nc.tensor.transpose(out=turned[:, 1, :], in_=exp_sum[:], identity=ident_f[:])
-        neg_max_t = turned[0:rows, 0, :].rearrange("r (d w) -> r d w", w=WIDTH)
-        exp_sum_t = turned[0:rows, 1, :].rearrange("r (d w) -> r d w", w=WIDTH)
+        turned_max = psum_t.tile([P, P], F32, tag="transposed")
+        nc.tensor.transpose(out=turned_max[:], in_=neg_max[:], identity=ident_f[:])
+        turned_sum = psum_t.tile([P, P], F32, tag="transposed")
+        nc.tensor.transpose(out=turned_sum[:], in_=exp_sum[:], identity=ident_f[:])
+        neg_max_t = turned_max[0:rows, :].rearrange("r (d w) -> r d w", w=WIDTH)
+        exp_sum_t = turned_sum[0:rows, :].rearrange("r (d w) -> r d w", w=WIDTH)
         shape = [rows, QUAD, WIDTH]
         neg_top = const.tile([rows, QUAD], F32)
         nc.vector.tensor_reduce(out=neg_top[:], in_=neg_max_t, axis=AXIS.X, op=ALU.min)

@@ -102,13 +102,17 @@ def tile_selfprojectiondev_pb_kernel(tc, x, o_xi, p_xi, rel_o_xi, out_0, out_1):
         p_raw = const.tile([P, DEPTHS, PACK * WIDTH], BF16)
         x_raws = []
 
-        def load_x(b):
+        def load_x(b, pieces=1):
             x_raw = x_in.tile([P, PACK, LENGTH], BF16)
-            nc.sync.dma_start(out=x_raw[:], in_=x[b].rearrange("(p j) c -> p j c", j=PACK))
+            rows_of_b = x[b].rearrange("(p j) c -> p j c", j=PACK)
+            width = LENGTH // pieces
+            for i in range(pieces):
+                cols = slice(i * width, (i + 1) * width)
+                nc.sync.dma_start(out=x_raw[:, :, cols], in_=rows_of_b[:, :, cols])
             x_raws.append(x_raw)
 
         nc.sync.dma_start(out=w_raw[:, 0], in_=o_xi.rearrange("d (p j) w -> p d (j w)", j=PACK))
-        load_x(0)
+        load_x(0, 2)
         nc.sync.dma_start(out=w_raw[:, 1], in_=rel_o_xi.rearrange("d (p j) w -> p d (j w)", j=PACK))
         load_x(1)
         load_x(2)
@@ -170,12 +174,15 @@ def tile_selfprojectiondev_pb_kernel(tc, x, o_xi, p_xi, rel_o_xi, out_0, out_1):
             )
             return bank
 
-        def regroup_x(b):
+        def regroup_x(b, pieces=1):
             x_grouped = x_work.tile([P, LENGTH, PACK], BF16, align_bytes=64)
-            nc.vector.tensor_copy(
-                out=x_grouped[:].rearrange("p (c i) j -> p c j i", i=4),
-                in_=x_raws[b][:].rearrange("p j (c i) -> p c j i", i=4),
-            )
+            width = LENGTH // pieces
+            for i in range(pieces):
+                cols = slice(i * width, (i + 1) * width)
+                nc.vector.tensor_copy(
+                    out=x_grouped[:, cols].rearrange("p (c i) j -> p c j i", i=4),
+                    in_=x_raws[b][:, :, cols].rearrange("p j (c i) -> p c j i", i=4),
+                )
             x_groupeds.append(x_grouped)
 
         def quantise_x(b):
@@ -185,47 +192,72 @@ def tile_selfprojectiondev_pb_kernel(tc, x, o_xi, p_xi, rel_o_xi, out_0, out_1):
             x_codes.append(codes)
             x_scales.append(scales)
 
+        CHAINS = ((0, 2), (2, 2), (4, 2), (6, 2))
         h_stats = []
+        chain_of = {}
+        for first, items in CHAINS:
+            h_stat = stats.tile([P, 2 * GROUPS * items], F32)
+            h_stats.append(h_stat)
+            for b in range(first, first + items):
+                chain_of[b] = (h_stat, first, items)
 
         def tanh_of_z(b):
-            if b % PAIR == 0:
-                h_stat = stats.tile([P, 2 * GROUPS * PAIR], F32)
-                h_stats.append(h_stat)
+            h_stat, first, items = chain_of[b]
             for g in range(GROUPS):
-                col = GROUPS * (b % PAIR) + g
+                col = GROUPS * (b - first) + g
                 z_bank = first_pass(g, b, "z")
                 h = h_pool.tile([P, 2, P, 2], F32)
                 nc.scalar.activation(
                     out=h[:],
                     in_=z_bank[:].rearrange("m (pj u e) -> m u pj e", u=2, e=2),
                     func=ACT.Tanh,
-                    accum_out=h_stats[b // PAIR][:, col : col + 1],
+                    accum_out=h_stat[:, col : col + 1],
                 )
                 h_tiles.append(h)
             for g in range(GROUPS):
-                col = GROUPS * (PAIR + b % PAIR) + g
-                h_squared = unread.tile([P, 2, P, 2], BF16, tag="unread")
-                nc.scalar.activation(
-                    out=h_squared[:],
-                    in_=h_tiles[GROUPS * b + g][:],
-                    func=ACT.Square,
-                    accum_out=h_stats[b // PAIR][:, col : col + 1],
-                )
+                if not square_on_vector(b, g):
+                    col = GROUPS * (items + b - first) + g
+                    h_squared = unread.tile([P, 2, P, 2], BF16, tag="unread")
+                    nc.scalar.activation(
+                        out=h_squared[:],
+                        in_=h_tiles[GROUPS * b + g][:],
+                        func=ACT.Square,
+                        accum_out=h_stat[:, col : col + 1],
+                    )
+
+        def square_on_vector(b, g):
+            return False
+
+        def square_of(b, g):
+            h_stat, first, items = chain_of[b]
+            col = GROUPS * (items + b - first) + g
+            h = h_tiles[GROUPS * b + g][:].rearrange("m u pj e -> m (u pj e)")
+            h_squared = unread.tile([P, LENGTH], BF16, tag="unread_v")
+            nc.vector.scalar_tensor_tensor(
+                out=h_squared[:],
+                in0=h,
+                scalar=1.0,
+                in1=h,
+                op0=ALU.mult,
+                op1=ALU.mult,
+                accum_out=h_stat[:, col : col + 1],
+            )
 
         from_roots = {}
 
-        def statistics_of_h(pair):
-            sets = GROUPS * PAIR
+        def statistics_of_h(chain):
+            first, items = CHAINS[chain]
+            sets = GROUPS * items
             h_totals = psum_small.tile([P, 2 * sets], F32, tag="small")
-            nc.tensor.matmul(out=h_totals[:], lhsT=quad_mean_h[:], rhs=h_stats[pair][:], start=True, stop=True)
+            nc.tensor.matmul(out=h_totals[:], lhsT=quad_mean_h[:], rhs=h_stats[chain][:], start=True, stop=True)
             h_mean, h_inverse, h_shift, to_root, from_root = statistics_steps(
                 nc, stats, h_totals, sets, LENGTH * WIDTH, half
             )
-            from_roots[pair] = from_root
+            from_roots[chain] = from_root
             for c in range(sets):
-                h_means[sets * pair + c] = h_mean[:, c : c + 1]
-                h_inverses[sets * pair + c] = h_inverse[:, c : c + 1]
-                h_shifts[sets * pair + c] = h_shift[:, c : c + 1]
+                h_means[GROUPS * first + c] = h_mean[:, c : c + 1]
+                h_inverses[GROUPS * first + c] = h_inverse[:, c : c + 1]
+                h_shifts[GROUPS * first + c] = h_shift[:, c : c + 1]
             return to_root
 
         r_banks = {}
@@ -268,12 +300,11 @@ def tile_selfprojectiondev_pb_kernel(tc, x, o_xi, p_xi, rel_o_xi, out_0, out_1):
         def quantise_p():
             quantise(nc, p_codes[:], p_scales[:], p_grouped[:].rearrange("p c j -> p (c j)"))
 
-        def place_p():
-            for source, target in ((p_codes[:].bitcast(I32), pz_codes[:].bitcast(I32)), (p_scales[:], pz_scales[:])):
-                nc.vector.tensor_copy(
-                    out=target.rearrange("p (d s) -> p d s", s=P + WIDTH)[:, :, 0:WIDTH],
-                    in_=source.rearrange("p (d w) -> p d w", w=WIDTH),
-                )
+        def place_p(source, target):
+            nc.vector.tensor_copy(
+                out=target.rearrange("p (d s) -> p d s", s=P + WIDTH)[:, :, 0:WIDTH],
+                in_=source.rearrange("p (d w) -> p d w", w=WIDTH),
+            )
 
         t_groupeds = {}
 
@@ -325,7 +356,9 @@ def tile_selfprojectiondev_pb_kernel(tc, x, o_xi, p_xi, rel_o_xi, out_0, out_1):
             quantise(nc, t_codes[:], t_scales[:], t_groupeds[rnd][:])
             t_operands[rnd] = (t_codes, t_scales)
 
-        def second_contraction(rnd):
+        u_banks = {}
+
+        def second_contraction_pass(rnd):
             t_codes, t_scales = t_operands[rnd]
             u_bank = psum_small.tile([P, GROUPS, ROUND * WIDTH], F32, tag="small")
             for g in range(GROUPS):
@@ -341,9 +374,12 @@ def tile_selfprojectiondev_pb_kernel(tc, x, o_xi, p_xi, rel_o_xi, out_0, out_1):
                         start=(q == 0),
                         stop=(q == QUAD - 1),
                     )
+            u_banks[rnd] = u_bank
+
+        def tanh_of_u(rnd):
             v_both = per_round.tile([P, 2 * SETS, WIDTH], F32)
             v = v_both[:, 0:SETS, :]
-            nc.scalar.activation(out=v, in_=u_bank[:].rearrange("m g (b w) -> m (g b) w", w=WIDTH), func=ACT.Tanh)
+            nc.scalar.activation(out=v, in_=u_banks[rnd][:].rearrange("m g (b w) -> m (g b) w", w=WIDTH), func=ACT.Tanh)
             nc.scalar.activation(out=v_both[:, SETS : 2 * SETS, :], in_=v, func=ACT.Square)
             v_tiles[rnd] = v_both
 
@@ -356,7 +392,7 @@ def tile_selfprojectiondev_pb_kernel(tc, x, o_xi, p_xi, rel_o_xi, out_0, out_1):
             nc.tensor.matmul(out=v_totals[:], lhsT=quad_mean_v[:], rhs=v_stat[:], start=True, stop=True)
             v_parts[rnd] = v_totals
 
-        def statistics_of_v(rnd):
+        def statistics_of_v(rnd, on_scalar):
             v_mean, v_inverse, v_shift, to_root, from_root = statistics_steps(
                 nc, stats, v_parts[rnd], SETS, WIDTH * WIDTH, half
             )
@@ -378,6 +414,9 @@ def tile_selfprojectiondev_pb_kernel(tc, x, o_xi, p_xi, rel_o_xi, out_0, out_1):
                     in1=v_inverse[:].unsqueeze(2).to_broadcast([P, SETS, WIDTH]),
                     op=ALU.mult,
                 )
+                store()
+
+            def store():
                 for g in range(GROUPS):
                     nc.sync.dma_start(
                         out=out_0[rnd * ROUND : (rnd + 1) * ROUND, g * QUAD : (g + 1) * QUAD].rearrange(
@@ -386,7 +425,53 @@ def tile_selfprojectiondev_pb_kernel(tc, x, o_xi, p_xi, rel_o_xi, out_0, out_1):
                         in_=proj[:, g * ROUND : (g + 1) * ROUND, :],
                     )
 
+            def standardise_on_scalar():
+                for s in range(SETS):
+                    nc.scalar.activation(
+                        out=proj[:, s, :],
+                        in_=v_tiles[rnd][:, s, :],
+                        func=ACT.Identity,
+                        scale=v_inverse[:, s : s + 1],
+                        bias=v_shift[:, s : s + 1],
+                    )
+                store()
+
+            if on_scalar:
+                return to_root, from_root + [standardise_on_scalar]
             return to_root + [centre], from_root[0:2] + [scale]
+
+        shape = [BATCH * GROUPS, QUAD, WIDTH]
+
+        def turned(statistic):
+            turned_tile = psum_t.tile([P, P], F32, tag="transposed")
+            nc.tensor.transpose(out=turned_tile[:], in_=statistic[:], identity=ident_f[:])
+            return turned_tile[0 : BATCH * GROUPS, :].rearrange("r (d w) -> r d w", w=WIDTH)
+
+        def weights_of_maxima():
+            neg_max_t = turned(neg_max)
+            neg_top = const.tile(shape[0:2], F32)
+            nc.vector.tensor_reduce(out=neg_top[:], in_=neg_max_t, axis=AXIS.X, op=ALU.min)
+            below_top = const.tile(shape, F32)
+            nc.vector.tensor_tensor(
+                out=below_top[:], in0=neg_top[:].unsqueeze(2).to_broadcast(shape), in1=neg_max_t, op=ALU.subtract
+            )
+            weight = const.tile(shape, F32)
+            nc.scalar.activation(out=weight[:], in_=below_top[:], func=ACT.Exp)
+            return weight
+
+        def store_mass(weight):
+            exp_sum_t = turned(exp_sum)
+            share = const.tile(shape, F32)
+            nc.vector.tensor_tensor(out=share[:], in0=weight[:], in1=exp_sum_t, op=ALU.mult)
+            whole = const.tile(shape[0:2], F32)
+            nc.vector.tensor_reduce(out=whole[:], in_=share[:], axis=AXIS.X, op=ALU.add)
+            whole_inverse = const.tile(shape[0:2], F32)
+            nc.vector.reciprocal(out=whole_inverse[:], in_=whole[:])
+            mass = const.tile(shape, F32)
+            nc.vector.tensor_tensor(
+                out=mass[:], in0=share[:], in1=whole_inverse[:].unsqueeze(2).to_broadcast(shape), op=ALU.mult
+            )
+            nc.sync.dma_start(out=out_1.rearrange("b (g d) w -> (b g) d w", g=GROUPS), in_=mass[:])
 
         V, S = nc.vector, nc.scalar
 
@@ -407,121 +492,103 @@ def tile_selfprojectiondev_pb_kernel(tc, x, o_xi, p_xi, rel_o_xi, out_0, out_1):
             for g in range(GROUPS):
                 exponentials(GROUPS * b + g)
 
+        places = [
+            later(place_p, p_codes[:].bitcast(I32), pz_codes[:].bitcast(I32)),
+            later(place_p, p_scales[:], pz_scales[:]),
+        ]
+
         stack.enter_context(tc.manual_schedule())
-        out, in_ = w_views(0)
-        nc.vector.tensor_copy(out=out, in_=in_)
+        for source in range(2):
+            out, in_ = w_views(source)
+            nc.scalar.copy(out=out, in_=in_)
+        regroup_x(0, 2)
         quantise_w(0)
-        out, in_ = w_views(1)
-        nc.scalar.copy(out=out, in_=in_)
-        regroup_x(0)
         quantise_x(0)
         tanh_of_z(0)
         regroup_x(1)
         quantise_w(1)
         quantise_x(1)
         tanh_of_z(1)
+        r_of(0)
         regroup_x(2)
         regroup_p()
         quantise_x(2)
         tanh_of_z(2)
+        before_0 = statistics_of_h(0)
         regroup_x(3)
         quantise_p()
         quantise_x(3)
-        to_root = statistics_of_h(0)
-        r_of(0)
         tanh_of_z(3)
-        weave(to_root[0:3], [later(regroup_x, 4), place_p, later(quantise_x, 4)])
+        weave(before_0[0:3], [later(regroup_x, 4), later(quantise_x, 4), later(regroup_x, 5), later(quantise_x, 5)])
         tanh_of_z(4)
-        regroup_x(5)
-        run(to_root[3:] + maxima(0))
-        regroup_x(6)
-        quantise_x(5)
-        to_root = statistics_of_h(1)
+        before_1 = statistics_of_h(1)
+        run(before_0[3:] + maxima(0))
         tanh_of_z(5)
-        run(from_roots[0])
-        regroup_x(7)
-        weave(to_root[0:3], rows(0, False, False))
+        run(before_1[0:1])
+        weave(from_roots[0][0:2], [later(regroup_x, 6)])
         quantise_x(6)
         tanh_of_z(6)
+        before_2 = statistics_of_h(2)
+        weave(before_1[1:3], rows(0, False, False) + [later(regroup_x, 7)])
         run(rows(1, False, False))
-        run(to_root[3:])
+        quantise_x(7)
+        tanh_of_z(7)
+        run(before_1[3:])
         group_t(0, V.tensor_copy)
         group_t(1, V.tensor_copy)
-        quantise_x(7)
-        to_root = statistics_of_h(2)
-        tanh_of_z(7)
-        weave(from_roots[1], to_root[0:3])
-        run(rows(2, False, False) + rows(3, False, False))
-        both_exponentials(0)
-        run(to_root[3:])
-        group_t(2, V.tensor_copy)
+        weave(from_roots[1][0:2], places)
+        weave(rows(2, False, False), before_2[0:2])
         r_of(1)
-        group_t(3, V.tensor_copy)
+        weave(rows(3, False, False), before_2[2:3])
+        before_3 = statistics_of_h(3)
+        both_exponentials(0)
+        run(before_2[3:])
+        group_t(2, V.tensor_copy)
         maximum(2)
-        to_root = statistics_of_h(3)
-        maximum(3)
+        group_t(3, V.tensor_copy)
         r_of(2)
         quantise_t(0)
-        second_contraction(0)
+        second_contraction_pass(0)
+        weave(from_roots[2] + before_3[0:1], maxima(1)[1:2])
         both_exponentials(1)
-        weave(to_root[0:3], from_roots[2])
-        run(to_root[3:] + maxima(2))
         r_of(3)
-        run(rows(4, False, True) + rows(5, False, True))
+        weave(before_3[1:3], rows(4, False, True) + maxima(2)[0:1])
+        run(before_3[3:] + maxima(2)[1:2])
         both_exponentials(2)
+        tanh_of_u(0)
+        run(maxima(3))
+        run(rows(5, False, True))
         group_t(4, S.copy)
-        sums_of_v(0)
-        group_t(5, S.copy)
-        weave(from_roots[3], maxima(3))
-        run(rows(6, False, True) + rows(7, False, True))
-        group_t(6, S.copy)
-        group_t(7, S.copy)
         r_of(4)
-        to_root, from_root = statistics_of_v(0)
-        weave(to_root[0:3], maxima(4))
+        weave(from_roots[3], [])
+        run(rows(6, False, True) + rows(7, False, True))
+        group_t(5, S.copy)
+        sums_of_v(0)
+        group_t(6, S.copy)
         both_exponentials(3)
+        group_t(7, V.tensor_copy)
+        steps, from_root = statistics_of_v(0, True)
+        run(steps[0:2] + maxima(4)[0:1])
         r_of(5)
         quantise_t(1)
-        second_contraction(1)
+        second_contraction_pass(1)
+        run(steps[2:3] + maxima(4)[1:2])
         both_exponentials(4)
-        run(to_root[3:4] + maxima(5))
-        r_of(6)
-        run(maxima(6)[0:1] + to_root[4:])
-        sums_of_v(1)
+        run(steps[3:] + maxima(5))
+        tanh_of_u(1)
         both_exponentials(5)
+        r_of(6)
+        run(maxima(6))
         r_of(7)
-        run(maxima(6)[1:2])
-        to_root_1, from_root_1 = statistics_of_v(1)
-        weave(to_root_1[0:4], from_root[0:2])
         both_exponentials(6)
-        run(maxima(7))
+        sums_of_v(1)
+        run(maxima(7)[0:1])
+        steps_1, from_root_1 = statistics_of_v(1, False)
+        weave(steps_1[0:3], from_root[0:3])
+        run(maxima(7)[1:2] + steps_1[4:])
         both_exponentials(7)
-        run(from_root[2:] + to_root_1[4:] + from_root_1)
-
-        rows = BATCH * GROUPS
-        turned_max = psum_t.tile([P, P], F32, tag="transposed")
-        nc.tensor.transpose(out=turned_max[:], in_=neg_max[:], identity=ident_f[:])
-        turned_sum = psum_t.tile([P, P], F32, tag="transposed")
-        nc.tensor.transpose(out=turned_sum[:], in_=exp_sum[:], identity=ident_f[:])
-        neg_max_t = turned_max[0:rows, :].rearrange("r (d w) -> r d w", w=WIDTH)
-        exp_sum_t = turned_sum[0:rows, :].rearrange("r (d w) -> r d w", w=WIDTH)
-        shape = [rows, QUAD, WIDTH]
-        neg_top = const.tile([rows, QUAD], F32)
-        nc.vector.tensor_reduce(out=neg_top[:], in_=neg_max_t, axis=AXIS.X, op=ALU.min)
-        below_top = const.tile(shape, F32)
-        nc.vector.tensor_tensor(
-            out=below_top[:], in0=neg_top[:].unsqueeze(2).to_broadcast(shape), in1=neg_max_t, op=ALU.subtract
-        )
-        weight = const.tile(shape, F32)
-        nc.scalar.activation(out=weight[:], in_=below_top[:], func=ACT.Exp)
-        share = const.tile(shape, F32)
-        nc.vector.tensor_tensor(out=share[:], in0=weight[:], in1=exp_sum_t, op=ALU.mult)
-        whole = const.tile([rows, QUAD], F32)
-        nc.vector.tensor_reduce(out=whole[:], in_=share[:], axis=AXIS.X, op=ALU.add)
-        whole_inverse = const.tile([rows, QUAD], F32)
-        nc.vector.reciprocal(out=whole_inverse[:], in_=whole[:])
-        mass = const.tile(shape, F32)
-        nc.vector.tensor_tensor(
-            out=mass[:], in0=share[:], in1=whole_inverse[:].unsqueeze(2).to_broadcast(shape), op=ALU.mult
-        )
-        nc.sync.dma_start(out=out_1.rearrange("b (g d) w -> (b g) d w", g=GROUPS), in_=mass[:])
+        run(from_root[3:])
+        run(steps_1[3:4])
+        weight = weights_of_maxima()
+        store_mass(weight)
+        run(from_root_1)

@@ -1,3 +1,4 @@
+import math
 from contextlib import ExitStack
 
 import concourse.mybir as mybir
@@ -35,8 +36,7 @@ def quantise(nc, codes, scales, grouped):
 
 
 def statistics_steps(nc, pool, totals, sets, count, half):
-    both = pool.tile([P, 2 * sets], F32, tag="both")
-    mean = both[:, 0:sets]
+    mean = pool.tile([P, sets], F32, tag="mean")
     mean_squared = pool.tile([P, sets], F32, tag="mean_squared")
     spread = pool.tile([P, sets], F32, tag="spread")
     variance = pool.tile([P, sets], F32, tag="variance")
@@ -45,33 +45,40 @@ def statistics_steps(nc, pool, totals, sets, count, half):
     inverse = pool.tile([P, sets], F32, tag="inverse")
     shift = pool.tile([P, sets], F32, tag="shift")
 
-    def read_totals():
-        nc.vector.tensor_copy(out=both[:], in_=totals[:])
+    def read_mean():
+        nc.vector.tensor_copy(out=mean[:], in_=totals[:, 0:sets])
 
     def square_mean():
-        nc.vector.tensor_tensor(out=mean_squared[:], in0=mean, in1=mean, op=ALU.mult)
-
-    def subtract():
-        nc.vector.tensor_tensor(out=spread[:], in0=both[:, sets : 2 * sets], in1=mean_squared[:], op=ALU.subtract)
+        nc.vector.tensor_tensor(out=mean_squared[:], in0=totals[:, 0:sets], in1=mean[:], op=ALU.mult)
 
     def root():
-        nc.vector.tensor_scalar(
-            out=variance[:], in0=spread[:], scalar1=count / (count - 1), scalar2=0.0, op0=ALU.mult, op1=ALU.max
+        nc.vector.tensor_tensor(
+            out=spread[:], in0=totals[:, sets : 2 * sets], in1=mean_squared[:], op=ALU.subtract
+        )
+        nc.gpsimd.tensor_scalar(
+            out=variance[:], in0=spread[:], scalar1=1.0, scalar2=0.0, op0=ALU.mult, op1=ALU.max
         )
         nc.gpsimd.tensor_tensor(out=std[:], in0=variance[:], in1=half[:, 0:sets], op=ALU.pow)
 
     def add_eps():
-        nc.vector.tensor_scalar(out=std_eps[:], in0=std[:], scalar1=1.0, scalar2=EPS, op0=ALU.mult, op1=ALU.add)
+        nc.vector.tensor_scalar(
+            out=std_eps[:],
+            in0=std[:],
+            scalar1=math.sqrt(count / (count - 1)),
+            scalar2=EPS,
+            op0=ALU.mult,
+            op1=ALU.add,
+        )
 
     def invert():
         nc.vector.reciprocal(out=inverse[:], in_=std_eps[:])
 
     def shift_step():
         nc.vector.scalar_tensor_tensor(
-            out=shift[:], in0=mean, scalar=-1.0, in1=inverse[:], op0=ALU.mult, op1=ALU.mult
+            out=shift[:], in0=mean[:], scalar=-1.0, in1=inverse[:], op0=ALU.mult, op1=ALU.mult
         )
 
-    return mean, inverse, shift, [read_totals, square_mean, subtract, root], [add_eps, invert, shift_step]
+    return mean, inverse, shift, [read_mean, square_mean, root], [add_eps, invert, shift_step]
 
 
 def weave(small, large):
@@ -91,7 +98,7 @@ def tile_selfprojectiondev_pb_kernel(tc, x, o_xi, p_xi, rel_o_xi, out_0, out_1):
         x_keep = stack.enter_context(tc.tile_pool(name="x_keep", bufs=BATCH))
         h_pool = stack.enter_context(tc.tile_pool(name="h_pool", bufs=GROUPS * BATCH))
         unread = stack.enter_context(tc.tile_pool(name="unread", bufs=4))
-        t_work = stack.enter_context(tc.tile_pool(name="t_work", bufs=4))
+        t_work = stack.enter_context(tc.tile_pool(name="t_work", bufs=2 * ROUND))
         per_round = stack.enter_context(tc.tile_pool(name="per_round", bufs=2))
         stats = stack.enter_context(tc.tile_pool(name="stats", bufs=6))
         psum_first = stack.enter_context(tc.psum_pool(name="psum_first", bufs=2))
@@ -102,17 +109,20 @@ def tile_selfprojectiondev_pb_kernel(tc, x, o_xi, p_xi, rel_o_xi, out_0, out_1):
         p_raw = const.tile([P, DEPTHS, PACK * WIDTH], BF16)
         x_raws = []
 
-        def load_x(b, pieces=1):
-            x_raw = x_in.tile([P, PACK, LENGTH], BF16)
-            rows_of_b = x[b].rearrange("(p j) c -> p j c", j=PACK)
-            width = LENGTH // pieces
-            for i in range(pieces):
-                cols = slice(i * width, (i + 1) * width)
-                nc.sync.dma_start(out=x_raw[:, :, cols], in_=rows_of_b[:, :, cols])
-            x_raws.append(x_raw)
+        def load_columns(b, cols):
+            nc.sync.dma_start(out=x_raws[b][:, :, cols], in_=x[b].rearrange("(p j) c -> p j c", j=PACK)[:, :, cols])
 
+        def load_x(b):
+            x_raw = x_in.tile([P, PACK, LENGTH], BF16)
+            x_raws.append(x_raw)
+            load_columns(b, slice(0, LENGTH))
+
+        first_x = x_in.tile([P, PACK, LENGTH], BF16, tag="x_raw")
+        x_raws.append(first_x)
+        split = LENGTH // 2
+        load_columns(0, slice(0, split))
         nc.sync.dma_start(out=w_raw[:, 0], in_=o_xi.rearrange("d (p j) w -> p d (j w)", j=PACK))
-        load_x(0, 2)
+        load_columns(0, slice(split, LENGTH))
         nc.sync.dma_start(out=w_raw[:, 1], in_=rel_o_xi.rearrange("d (p j) w -> p d (j w)", j=PACK))
         load_x(1)
         load_x(2)
@@ -174,26 +184,25 @@ def tile_selfprojectiondev_pb_kernel(tc, x, o_xi, p_xi, rel_o_xi, out_0, out_1):
             )
             return bank
 
-        def regroup_x(b, pieces=1):
-            x_grouped = x_work.tile([P, LENGTH, PACK], BF16, align_bytes=64)
-            width = LENGTH // pieces
-            for i in range(pieces):
-                cols = slice(i * width, (i + 1) * width)
-                nc.vector.tensor_copy(
-                    out=x_grouped[:, cols].rearrange("p (c i) j -> p c j i", i=4),
-                    in_=x_raws[b][:, :, cols].rearrange("p j (c i) -> p c j i", i=4),
-                )
-            x_groupeds.append(x_grouped)
+        def regroup_x(b, cols=slice(0, LENGTH)):
+            if b == len(x_groupeds):
+                x_grouped = x_work.tile([P, LENGTH, PACK], BF16, align_bytes=64)
+                x_groupeds.append(x_grouped)
+            nc.vector.tensor_copy(
+                out=x_groupeds[b][:, cols].rearrange("p (c i) j -> p c j i", i=4),
+                in_=x_raws[b][:, :, cols].rearrange("p j (c i) -> p c j i", i=4),
+            )
 
-        def quantise_x(b):
-            codes = x_keep.tile([P, LENGTH], U32, align_bytes=64)
-            scales = x_keep.tile([P, LENGTH], U8, align_bytes=64)
-            quantise(nc, codes[:], scales[:], x_groupeds[b][:].rearrange("p c j -> p (c j)"))
-            x_codes.append(codes)
-            x_scales.append(scales)
+        def quantise_x(b, cols=slice(0, LENGTH)):
+            if b == len(x_codes):
+                codes = x_keep.tile([P, LENGTH], U32, align_bytes=64)
+                scales = x_keep.tile([P, LENGTH], U8, align_bytes=64)
+                x_codes.append(codes)
+                x_scales.append(scales)
+            quantise(nc, x_codes[b][:, cols], x_scales[b][:, cols], x_groupeds[b][:, cols].rearrange("p c j -> p (c j)"))
 
-        CHAINS = ((0, 2), (2, 2), (4, 2), (6, 2))
         h_stats = []
+        CHAINS = ((0, 2), (2, 2), (4, 4))
         chain_of = {}
         for first, items in CHAINS:
             h_stat = stats.tile([P, 2 * GROUPS * items], F32)
@@ -215,33 +224,14 @@ def tile_selfprojectiondev_pb_kernel(tc, x, o_xi, p_xi, rel_o_xi, out_0, out_1):
                 )
                 h_tiles.append(h)
             for g in range(GROUPS):
-                if not square_on_vector(b, g):
-                    col = GROUPS * (items + b - first) + g
-                    h_squared = unread.tile([P, 2, P, 2], BF16, tag="unread")
-                    nc.scalar.activation(
-                        out=h_squared[:],
-                        in_=h_tiles[GROUPS * b + g][:],
-                        func=ACT.Square,
-                        accum_out=h_stat[:, col : col + 1],
-                    )
-
-        def square_on_vector(b, g):
-            return False
-
-        def square_of(b, g):
-            h_stat, first, items = chain_of[b]
-            col = GROUPS * (items + b - first) + g
-            h = h_tiles[GROUPS * b + g][:].rearrange("m u pj e -> m (u pj e)")
-            h_squared = unread.tile([P, LENGTH], BF16, tag="unread_v")
-            nc.vector.scalar_tensor_tensor(
-                out=h_squared[:],
-                in0=h,
-                scalar=1.0,
-                in1=h,
-                op0=ALU.mult,
-                op1=ALU.mult,
-                accum_out=h_stat[:, col : col + 1],
-            )
+                col = GROUPS * (items + b - first) + g
+                h_squared = unread.tile([P, 2, P, 2], BF16, tag="unread")
+                nc.scalar.activation(
+                    out=h_squared[:],
+                    in_=h_tiles[GROUPS * b + g][:],
+                    func=ACT.Square,
+                    accum_out=h_stat[:, col : col + 1],
+                )
 
         from_roots = {}
 
@@ -348,6 +338,7 @@ def tile_selfprojectiondev_pb_kernel(tc, x, o_xi, p_xi, rel_o_xi, out_0, out_1):
             copy(out=words[:, :, bi], in_=turned_t[b][:].rearrange("p u (d w) -> p d w u", w=WIDTH))
 
         v_tiles = {}
+        v_stats = {}
         t_operands = {}
 
         def quantise_t(rnd):
@@ -377,19 +368,26 @@ def tile_selfprojectiondev_pb_kernel(tc, x, o_xi, p_xi, rel_o_xi, out_0, out_1):
             u_banks[rnd] = u_bank
 
         def tanh_of_u(rnd):
-            v_both = per_round.tile([P, 2 * SETS, WIDTH], F32)
-            v = v_both[:, 0:SETS, :]
-            nc.scalar.activation(out=v, in_=u_banks[rnd][:].rearrange("m g (b w) -> m (g b) w", w=WIDTH), func=ACT.Tanh)
-            nc.scalar.activation(out=v_both[:, SETS : 2 * SETS, :], in_=v, func=ACT.Square)
-            v_tiles[rnd] = v_both
+            v = per_round.tile([P, SETS, WIDTH], F32)
+            v_stat = per_round.tile([P, 2 * SETS], F32)
+            u = u_banks[rnd][:].rearrange("m g (b w) -> m (g b) w", w=WIDTH)
+            for s in range(SETS):
+                nc.scalar.activation(
+                    out=v[:, s, :], in_=u[:, s, :], func=ACT.Tanh, accum_out=v_stat[:, s : s + 1]
+                )
+            for s in range(SETS):
+                v_squared = unread.tile([P, WIDTH], BF16, tag="unread_v")
+                nc.scalar.activation(
+                    out=v_squared[:], in_=v[:, s, :], func=ACT.Square, accum_out=v_stat[:, SETS + s : SETS + s + 1]
+                )
+            v_tiles[rnd] = v
+            v_stats[rnd] = v_stat
 
         v_parts = {}
 
         def sums_of_v(rnd):
-            v_stat = per_round.tile([P, 2 * SETS], F32)
-            nc.vector.tensor_reduce(out=v_stat[:], in_=v_tiles[rnd][:], axis=AXIS.X, op=ALU.add)
             v_totals = psum_small.tile([P, 2 * SETS], F32, tag="small")
-            nc.tensor.matmul(out=v_totals[:], lhsT=quad_mean_v[:], rhs=v_stat[:], start=True, stop=True)
+            nc.tensor.matmul(out=v_totals[:], lhsT=quad_mean_v[:], rhs=v_stats[rnd][:], start=True, stop=True)
             v_parts[rnd] = v_totals
 
         def statistics_of_v(rnd, on_scalar):
@@ -402,8 +400,8 @@ def tile_selfprojectiondev_pb_kernel(tc, x, o_xi, p_xi, rel_o_xi, out_0, out_1):
             def centre():
                 nc.vector.tensor_tensor(
                     out=centred[:],
-                    in0=v_tiles[rnd][:, 0:SETS, :],
-                    in1=v_mean.unsqueeze(2).to_broadcast([P, SETS, WIDTH]),
+                    in0=v_tiles[rnd][:],
+                    in1=v_mean[:].unsqueeze(2).to_broadcast([P, SETS, WIDTH]),
                     op=ALU.subtract,
                 )
 
@@ -438,7 +436,7 @@ def tile_selfprojectiondev_pb_kernel(tc, x, o_xi, p_xi, rel_o_xi, out_0, out_1):
 
             if on_scalar:
                 return to_root, from_root + [standardise_on_scalar]
-            return to_root + [centre], from_root[0:2] + [scale]
+            return to_root, [from_root[0], centre, from_root[1], scale]
 
         shape = [BATCH * GROUPS, QUAD, WIDTH]
 
@@ -459,19 +457,29 @@ def tile_selfprojectiondev_pb_kernel(tc, x, o_xi, p_xi, rel_o_xi, out_0, out_1):
             nc.scalar.activation(out=weight[:], in_=below_top[:], func=ACT.Exp)
             return weight
 
-        def store_mass(weight):
+        def mass_steps(weight):
             exp_sum_t = turned(exp_sum)
             share = const.tile(shape, F32)
-            nc.vector.tensor_tensor(out=share[:], in0=weight[:], in1=exp_sum_t, op=ALU.mult)
             whole = const.tile(shape[0:2], F32)
-            nc.vector.tensor_reduce(out=whole[:], in_=share[:], axis=AXIS.X, op=ALU.add)
             whole_inverse = const.tile(shape[0:2], F32)
-            nc.vector.reciprocal(out=whole_inverse[:], in_=whole[:])
             mass = const.tile(shape, F32)
-            nc.vector.tensor_tensor(
-                out=mass[:], in0=share[:], in1=whole_inverse[:].unsqueeze(2).to_broadcast(shape), op=ALU.mult
-            )
-            nc.sync.dma_start(out=out_1.rearrange("b (g d) w -> (b g) d w", g=GROUPS), in_=mass[:])
+
+            def weigh():
+                nc.vector.tensor_tensor(out=share[:], in0=weight[:], in1=exp_sum_t, op=ALU.mult)
+
+            def add_up():
+                nc.vector.tensor_reduce(out=whole[:], in_=share[:], axis=AXIS.X, op=ALU.add)
+
+            def invert_whole():
+                nc.vector.reciprocal(out=whole_inverse[:], in_=whole[:])
+
+            def store():
+                nc.vector.tensor_tensor(
+                    out=mass[:], in0=share[:], in1=whole_inverse[:].unsqueeze(2).to_broadcast(shape), op=ALU.mult
+                )
+                nc.sync.dma_start(out=out_1.rearrange("b (g d) w -> (b g) d w", g=GROUPS), in_=mass[:])
+
+            return [weigh, add_up, invert_whole, store]
 
         V, S = nc.vector, nc.scalar
 
@@ -501,9 +509,11 @@ def tile_selfprojectiondev_pb_kernel(tc, x, o_xi, p_xi, rel_o_xi, out_0, out_1):
         for source in range(2):
             out, in_ = w_views(source)
             nc.scalar.copy(out=out, in_=in_)
-        regroup_x(0, 2)
+        regroup_x(0, slice(0, split))
+        quantise_x(0, slice(0, split))
+        regroup_x(0, slice(split, LENGTH))
         quantise_w(0)
-        quantise_x(0)
+        quantise_x(0, slice(split, LENGTH))
         tanh_of_z(0)
         regroup_x(1)
         quantise_w(1)
@@ -519,76 +529,74 @@ def tile_selfprojectiondev_pb_kernel(tc, x, o_xi, p_xi, rel_o_xi, out_0, out_1):
         quantise_p()
         quantise_x(3)
         tanh_of_z(3)
-        weave(before_0[0:3], [later(regroup_x, 4), later(quantise_x, 4), later(regroup_x, 5), later(quantise_x, 5)])
+        regroup_x(4)
+        weave(before_0[0:2], [later(quantise_x, 4), later(regroup_x, 5)])
         tanh_of_z(4)
         before_1 = statistics_of_h(1)
-        run(before_0[3:] + maxima(0))
+        run(before_0[2:] + maxima(0))
+        quantise_x(5)
         tanh_of_z(5)
-        run(before_1[0:1])
-        weave(from_roots[0][0:2], [later(regroup_x, 6)])
-        quantise_x(6)
+        regroup_x(6)
+        weave(from_roots[0][0:2], [later(quantise_x, 6)] + before_1[0:1])
         tanh_of_z(6)
-        before_2 = statistics_of_h(2)
-        weave(before_1[1:3], rows(0, False, False) + [later(regroup_x, 7)])
+        weave(before_1[1:2], rows(0, False, False) + [later(regroup_x, 7)])
         run(rows(1, False, False))
         quantise_x(7)
         tanh_of_z(7)
-        run(before_1[3:])
+        run(before_1[2:])
         group_t(0, V.tensor_copy)
         group_t(1, V.tensor_copy)
         weave(from_roots[1][0:2], places)
-        weave(rows(2, False, False), before_2[0:2])
         r_of(1)
-        weave(rows(3, False, False), before_2[2:3])
-        before_3 = statistics_of_h(3)
-        both_exponentials(0)
-        run(before_2[3:])
-        group_t(2, V.tensor_copy)
+        run(rows(2, False, False))
+        before_2 = statistics_of_h(2)
+        run(rows(3, False, False))
         maximum(2)
-        group_t(3, V.tensor_copy)
+        both_exponentials(0)
         r_of(2)
-        quantise_t(0)
-        second_contraction_pass(0)
-        weave(from_roots[2] + before_3[0:1], maxima(1)[1:2])
+        group_t(2, S.copy)
+        group_t(3, S.copy)
+        run(before_2 + maxima(1)[1:2] + maxima(2))
         both_exponentials(1)
         r_of(3)
-        weave(before_3[1:3], rows(4, False, True) + maxima(2)[0:1])
-        run(before_3[3:] + maxima(2)[1:2])
+        run(maxima(3)[0:1])
         both_exponentials(2)
-        tanh_of_u(0)
-        run(maxima(3))
-        run(rows(5, False, True))
+        run(from_roots[2])
+        run(rows(4, False, False) + rows(5, False, False) + rows(6, False, True))
         group_t(4, S.copy)
-        r_of(4)
-        weave(from_roots[3], [])
-        run(rows(6, False, True) + rows(7, False, True))
+        run(rows(7, False, True))
         group_t(5, S.copy)
-        sums_of_v(0)
         group_t(6, S.copy)
-        both_exponentials(3)
+        quantise_t(0)
         group_t(7, V.tensor_copy)
-        steps, from_root = statistics_of_v(0, True)
-        run(steps[0:2] + maxima(4)[0:1])
-        r_of(5)
+        second_contraction_pass(0)
+        exponentials(6)
+        r_of(4)
+        tanh_of_u(0)
         quantise_t(1)
         second_contraction_pass(1)
-        run(steps[2:3] + maxima(4)[1:2])
-        both_exponentials(4)
-        run(steps[3:] + maxima(5))
+        run(maxima(3)[1:2])
+        exponentials(7)
+        sums_of_v(0)
+        r_of(5)
+        run(maxima(4)[0:1])
         tanh_of_u(1)
-        both_exponentials(5)
-        r_of(6)
-        run(maxima(6))
-        r_of(7)
-        both_exponentials(6)
+        exponentials(8)
+        steps, from_root = statistics_of_v(0, True)
+        run(steps + maxima(4)[1:2])
+        exponentials(9)
         sums_of_v(1)
-        run(maxima(7)[0:1])
+        run(maxima(5))
+        r_of(6)
         steps_1, from_root_1 = statistics_of_v(1, False)
-        weave(steps_1[0:3], from_root[0:3])
-        run(maxima(7)[1:2] + steps_1[4:])
+        both_exponentials(5)
+        r_of(7)
+        weave(steps_1[0:2], maxima(6)[0:1])
+        run(from_root[0:3] + steps_1[2:])
+        run(maxima(6)[1:2] + maxima(7))
+        both_exponentials(6)
         both_exponentials(7)
         run(from_root[3:])
-        run(steps_1[3:4])
         weight = weights_of_maxima()
-        store_mass(weight)
-        run(from_root_1)
+        run(from_root_1[0:2])
+        weave(mass_steps(weight), from_root_1[2:])

@@ -1,4 +1,3 @@
-import math
 from contextlib import ExitStack
 
 import concourse.mybir as mybir
@@ -51,24 +50,19 @@ def statistics_steps(nc, pool, totals, sets, count, half):
     def square_mean():
         nc.vector.tensor_tensor(out=mean_squared[:], in0=totals[:, 0:sets], in1=mean[:], op=ALU.mult)
 
-    def root():
+    def subtract():
         nc.vector.tensor_tensor(
             out=spread[:], in0=totals[:, sets : 2 * sets], in1=mean_squared[:], op=ALU.subtract
         )
-        nc.gpsimd.tensor_scalar(
-            out=variance[:], in0=spread[:], scalar1=1.0, scalar2=0.0, op0=ALU.mult, op1=ALU.max
+
+    def root():
+        nc.vector.tensor_scalar(
+            out=variance[:], in0=spread[:], scalar1=count / (count - 1), scalar2=0.0, op0=ALU.mult, op1=ALU.max
         )
         nc.gpsimd.tensor_tensor(out=std[:], in0=variance[:], in1=half[:, 0:sets], op=ALU.pow)
 
     def add_eps():
-        nc.vector.tensor_scalar(
-            out=std_eps[:],
-            in0=std[:],
-            scalar1=math.sqrt(count / (count - 1)),
-            scalar2=EPS,
-            op0=ALU.mult,
-            op1=ALU.add,
-        )
+        nc.vector.tensor_scalar_add(out=std_eps[:], in0=std[:], scalar1=EPS)
 
     def invert():
         nc.vector.reciprocal(out=inverse[:], in_=std_eps[:])
@@ -78,7 +72,7 @@ def statistics_steps(nc, pool, totals, sets, count, half):
             out=shift[:], in0=mean[:], scalar=-1.0, in1=inverse[:], op0=ALU.mult, op1=ALU.mult
         )
 
-    return mean, inverse, shift, [read_mean, square_mean, root], [add_eps, invert, shift_step]
+    return mean, inverse, shift, [read_mean, square_mean, subtract, root], [add_eps, invert, shift_step]
 
 
 def weave(small, large):
@@ -102,7 +96,7 @@ def tile_selfprojectiondev_pb_kernel(tc, x, o_xi, p_xi, rel_o_xi, out_0, out_1):
         per_round = stack.enter_context(tc.tile_pool(name="per_round", bufs=2))
         stats = stack.enter_context(tc.tile_pool(name="stats", bufs=6))
         psum_first = stack.enter_context(tc.psum_pool(name="psum_first", bufs=2))
-        psum_t = stack.enter_context(tc.psum_pool(name="psum_t", bufs=3))
+        psum_t = stack.enter_context(tc.psum_pool(name="psum_t", bufs=2))
         psum_small = stack.enter_context(tc.psum_pool(name="psum_small", bufs=1))
 
         w_raw = const.tile([P, 2, DEPTHS, PACK * WIDTH], BF16)
@@ -172,7 +166,7 @@ def tile_selfprojectiondev_pb_kernel(tc, x, o_xi, p_xi, rel_o_xi, out_0, out_1):
 
         def first_pass(operand, b, tag):
             own = slice(operand * P, (operand + 1) * P)
-            bank = psum_first.tile([P, LENGTH], F32, tag=tag)
+            bank = psum_first.tile([P, LENGTH], F32, tag=tag, bufs=3 if tag == "r" else 2)
             nc.tensor.matmul_mx(
                 out=bank[:],
                 lhsT=w_codes[:, own].bitcast(FP8X4),
@@ -254,8 +248,11 @@ def tile_selfprojectiondev_pb_kernel(tc, x, o_xi, p_xi, rel_o_xi, out_0, out_1):
 
         def r_of(b):
             for g in range(GROUPS):
-                r_bank = first_pass(GROUPS + g, b, "r" if b % 2 == 0 else "z")
-                r_banks[GROUPS * b + g] = r_bank
+                r_column(GROUPS * b + g)
+
+        def r_column(col):
+            r_bank = first_pass(GROUPS + col % GROUPS, col // GROUPS, "r" if col % 5 < 3 else "z")
+            r_banks[col] = r_bank
 
         def maximum(col):
             nc.vector.tensor_reduce(
@@ -540,29 +537,33 @@ def tile_selfprojectiondev_pb_kernel(tc, x, o_xi, p_xi, rel_o_xi, out_0, out_1):
         weave(from_roots[0][0:2], [later(quantise_x, 6)] + before_1[0:1])
         tanh_of_z(6)
         weave(before_1[1:2], rows(0, False, False) + [later(regroup_x, 7)])
-        run(rows(1, False, False))
+        run(rows(1, False, False)[0:1])
         quantise_x(7)
         tanh_of_z(7)
+        run(rows(1, False, False)[1:])
         run(before_1[2:])
+        r_column(2)
         group_t(0, V.tensor_copy)
         group_t(1, V.tensor_copy)
-        weave(from_roots[1][0:2], places)
-        r_of(1)
-        run(rows(2, False, False))
-        before_2 = statistics_of_h(2)
-        run(rows(3, False, False))
         maximum(2)
+        weave(from_roots[1][0:2], places)
+        r_column(3)
+        before_2 = statistics_of_h(2)
+        r_column(4)
+        run(rows(2, False, False))
+        weave(before_2[0:3], rows(3, False, False))
         both_exponentials(0)
-        r_of(2)
+        r_column(5)
         group_t(2, S.copy)
         group_t(3, S.copy)
-        run(before_2 + maxima(1)[1:2] + maxima(2))
+        run(before_2[3:] + maxima(1)[1:2] + maxima(2))
         both_exponentials(1)
         r_of(3)
-        run(maxima(3)[0:1])
+        run(maxima(3))
         both_exponentials(2)
-        run(from_roots[2])
-        run(rows(4, False, False) + rows(5, False, False) + rows(6, False, True))
+        run(from_roots[2][0:2])
+        weave(rows(4, False, False), from_roots[2][2:])
+        run(rows(5, False, False) + rows(6, False, True))
         group_t(4, S.copy)
         run(rows(7, False, True))
         group_t(5, S.copy)
@@ -575,28 +576,25 @@ def tile_selfprojectiondev_pb_kernel(tc, x, o_xi, p_xi, rel_o_xi, out_0, out_1):
         tanh_of_u(0)
         quantise_t(1)
         second_contraction_pass(1)
-        run(maxima(3)[1:2])
-        exponentials(7)
         sums_of_v(0)
+        exponentials(7)
         r_of(5)
-        run(maxima(4)[0:1])
+        run(maxima(4))
         tanh_of_u(1)
         exponentials(8)
         steps, from_root = statistics_of_v(0, True)
-        run(steps + maxima(4)[1:2])
+        run(steps + maxima(5)[0:1])
         exponentials(9)
         sums_of_v(1)
-        run(maxima(5))
         r_of(6)
+        run(maxima(5)[1:2])
         steps_1, from_root_1 = statistics_of_v(1, False)
-        both_exponentials(5)
         r_of(7)
-        weave(steps_1[0:2], maxima(6)[0:1])
-        run(from_root[0:3] + steps_1[2:])
-        run(maxima(6)[1:2] + maxima(7))
+        weave(steps_1, maxima(6))
+        both_exponentials(5)
+        run(maxima(7))
         both_exponentials(6)
         both_exponentials(7)
-        run(from_root[3:])
         weight = weights_of_maxima()
-        run(from_root_1[0:2])
+        run(from_root[0:1] + from_root_1[0:1] + from_root[1:2] + from_root_1[1:2] + from_root[2:])
         weave(mass_steps(weight), from_root_1[2:])

@@ -25,6 +25,7 @@ ROUND = 4
 SETS = GROUPS * ROUND
 PAIR = 2
 EPS = 1e-5
+OPERANDS = 4
 SPAN = QUAD * (P + WIDTH)
 
 FLOPS = 2 * BATCH * DEPTHS * (2 * LENGTH * LENGTH * WIDTH + LENGTH * WIDTH * WIDTH)
@@ -99,29 +100,34 @@ def tile_selfprojectiondev_pb_kernel(tc, x, o_xi, p_xi, rel_o_xi, out_0, out_1):
         psum_t = stack.enter_context(tc.psum_pool(name="psum_t", bufs=2))
         psum_small = stack.enter_context(tc.psum_pool(name="psum_small", bufs=1))
 
-        w_raw = const.tile([P, 2, DEPTHS, PACK * WIDTH], BF16)
+        w_raw = const.tile([P, OPERANDS, QUAD, PACK * WIDTH], BF16)
         p_raw = const.tile([P, DEPTHS, PACK * WIDTH], BF16)
         x_raws = []
 
-        def load_columns(b, cols):
-            nc.sync.dma_start(out=x_raws[b][:, :, cols], in_=x[b].rearrange("(p j) c -> p j c", j=PACK)[:, :, cols])
+        def load_x(b, rows=slice(0, PACK)):
+            if b == len(x_raws):
+                x_raw = x_in.tile([P, PACK, LENGTH], BF16)
+                x_raws.append(x_raw)
+            nc.sync.dma_start(out=x_raws[b][:, rows], in_=x[b].rearrange("(p j) c -> p j c", j=PACK)[:, rows])
 
-        def load_x(b):
-            x_raw = x_in.tile([P, PACK, LENGTH], BF16)
-            x_raws.append(x_raw)
-            load_columns(b, slice(0, LENGTH))
+        def load_w(n):
+            source = o_xi if n < GROUPS else rel_o_xi
+            g = n % GROUPS
+            nc.sync.dma_start(
+                out=w_raw[:, n], in_=source[g * QUAD : (g + 1) * QUAD].rearrange("d (p j) w -> p d (j w)", j=PACK)
+            )
 
-        first_x = x_in.tile([P, PACK, LENGTH], BF16, tag="x_raw")
-        x_raws.append(first_x)
-        split = LENGTH // 2
-        load_columns(0, slice(0, split))
-        nc.sync.dma_start(out=w_raw[:, 0], in_=o_xi.rearrange("d (p j) w -> p d (j w)", j=PACK))
-        load_columns(0, slice(split, LENGTH))
-        nc.sync.dma_start(out=w_raw[:, 1], in_=rel_o_xi.rearrange("d (p j) w -> p d (j w)", j=PACK))
+        load_x(0, slice(0, 2))
+        load_x(0, slice(2, PACK))
+        load_w(0)
+        load_w(1)
         load_x(1)
+        load_w(2)
+        load_w(3)
         load_x(2)
+        load_x(3)
         nc.sync.dma_start(out=p_raw[:], in_=p_xi.rearrange("d (p j) w -> p d (j w)", j=PACK))
-        for b in range(3, BATCH):
+        for b in range(4, BATCH):
             load_x(b)
 
         half = const.tile([P, SETS], F32)
@@ -142,19 +148,21 @@ def tile_selfprojectiondev_pb_kernel(tc, x, o_xi, p_xi, rel_o_xi, out_0, out_1):
         exp_sum = const.tile([P, P], F32)
         nc.vector.memset(exp_sum[:], 0.0)
 
-        w_grouped = const.tile([P, 2, DEPTHS * WIDTH, PACK], BF16, align_bytes=64)
-        w_codes = const.tile([P, 2 * DEPTHS * WIDTH], U32, align_bytes=64)
-        w_scales = const.tile([P, 2 * DEPTHS * WIDTH], U8, align_bytes=64)
+        w_grouped = const.tile([P, OPERANDS, P, PACK], BF16, align_bytes=64)
+        w_codes = const.tile([P, OPERANDS * P], U32, align_bytes=64)
+        w_scales = const.tile([P, OPERANDS * P], U8, align_bytes=64)
 
-        def w_views(source):
-            return (
-                w_grouped[:, source].rearrange("p (d w) j -> p d w j", w=WIDTH),
-                w_raw[:, source].rearrange("p d (j w) -> p d w j", j=PACK),
+        def regroup_w(n, copy):
+            copy(
+                out=w_grouped[:, n].rearrange("p (d w) j -> p d w j", w=WIDTH),
+                in_=w_raw[:, n].rearrange("p d (j w) -> p d w j", j=PACK),
             )
 
-        def quantise_w(source):
-            own = slice(source * DEPTHS * WIDTH, (source + 1) * DEPTHS * WIDTH)
-            quantise(nc, w_codes[:, own], w_scales[:, own], w_grouped[:, source].rearrange("p c j -> p (c j)"))
+        def quantise_w(first, last):
+            own = slice(first * P, (last + 1) * P)
+            quantise(
+                nc, w_codes[:, own], w_scales[:, own], w_grouped[:, first : last + 1].rearrange("p n c j -> p (n c j)")
+            )
 
         x_groupeds = []
         x_codes = []
@@ -178,25 +186,24 @@ def tile_selfprojectiondev_pb_kernel(tc, x, o_xi, p_xi, rel_o_xi, out_0, out_1):
             )
             return bank
 
-        def regroup_x(b, cols=slice(0, LENGTH)):
+        def regroup_x(b, rows=slice(0, PACK)):
             if b == len(x_groupeds):
                 x_grouped = x_work.tile([P, LENGTH, PACK], BF16, align_bytes=64)
                 x_groupeds.append(x_grouped)
             nc.vector.tensor_copy(
-                out=x_groupeds[b][:, cols].rearrange("p (c i) j -> p c j i", i=4),
-                in_=x_raws[b][:, :, cols].rearrange("p j (c i) -> p c j i", i=4),
+                out=x_groupeds[b][:, :, rows].rearrange("p (c i) j -> p c j i", i=4),
+                in_=x_raws[b][:, rows].rearrange("p j (c i) -> p c j i", i=4),
             )
 
-        def quantise_x(b, cols=slice(0, LENGTH)):
-            if b == len(x_codes):
-                codes = x_keep.tile([P, LENGTH], U32, align_bytes=64)
-                scales = x_keep.tile([P, LENGTH], U8, align_bytes=64)
-                x_codes.append(codes)
-                x_scales.append(scales)
-            quantise(nc, x_codes[b][:, cols], x_scales[b][:, cols], x_groupeds[b][:, cols].rearrange("p c j -> p (c j)"))
+        def quantise_x(b):
+            codes = x_keep.tile([P, LENGTH], U32, align_bytes=64)
+            scales = x_keep.tile([P, LENGTH], U8, align_bytes=64)
+            x_codes.append(codes)
+            x_scales.append(scales)
+            quantise(nc, codes[:], scales[:], x_groupeds[b][:].rearrange("p c j -> p (c j)"))
 
         h_stats = []
-        CHAINS = ((0, 2), (2, 2), (4, 4))
+        CHAINS = ((0, 2), (2, 4), (6, 2))
         chain_of = {}
         for first, items in CHAINS:
             h_stat = stats.tile([P, 2 * GROUPS * items], F32)
@@ -503,96 +510,103 @@ def tile_selfprojectiondev_pb_kernel(tc, x, o_xi, p_xi, rel_o_xi, out_0, out_1):
         ]
 
         stack.enter_context(tc.manual_schedule())
-        for source in range(2):
-            out, in_ = w_views(source)
-            nc.scalar.copy(out=out, in_=in_)
-        regroup_x(0, slice(0, split))
-        quantise_x(0, slice(0, split))
-        regroup_x(0, slice(split, LENGTH))
-        quantise_w(0)
-        quantise_x(0, slice(split, LENGTH))
+        regroup_x(0, slice(0, 2))
+        regroup_x(0, slice(2, PACK))
+        regroup_w(0, S.copy)
+        regroup_w(1, S.copy)
+        quantise_x(0)
+        quantise_w(0, 0)
+        quantise_w(1, 1)
         tanh_of_z(0)
         regroup_x(1)
-        quantise_w(1)
+        regroup_w(2, V.tensor_copy)
         quantise_x(1)
         tanh_of_z(1)
-        r_of(0)
+        regroup_w(3, V.tensor_copy)
         regroup_x(2)
-        regroup_p()
+        quantise_w(2, 3)
         quantise_x(2)
         tanh_of_z(2)
         before_0 = statistics_of_h(0)
+        r_of(0)
         regroup_x(3)
-        quantise_p()
+        regroup_p()
         quantise_x(3)
         tanh_of_z(3)
+        quantise_p()
         regroup_x(4)
         weave(before_0[0:2], [later(quantise_x, 4), later(regroup_x, 5)])
         tanh_of_z(4)
-        before_1 = statistics_of_h(1)
-        run(before_0[2:] + maxima(0))
+        run(before_0[2:3])
         quantise_x(5)
         tanh_of_z(5)
+        run(before_0[3:] + maxima(0))
         regroup_x(6)
-        weave(from_roots[0][0:2], [later(quantise_x, 6)] + before_1[0:1])
+        weave(from_roots[0][0:2], [later(quantise_x, 6)])
         tanh_of_z(6)
-        weave(before_1[1:2], rows(0, False, False) + [later(regroup_x, 7)])
-        run(rows(1, False, False)[0:1])
+        before_1 = statistics_of_h(1)
+        run(rows(0, False, False)[0:1])
+        regroup_x(7)
+        run(rows(0, False, False)[1:])
         quantise_x(7)
         tanh_of_z(7)
-        run(rows(1, False, False)[1:])
-        run(before_1[2:])
+        weave(before_1, rows(1, False, False))
         r_column(2)
         group_t(0, V.tensor_copy)
         group_t(1, V.tensor_copy)
         maximum(2)
-        weave(from_roots[1][0:2], places)
         r_column(3)
+        maximum(3)
+        weave(from_roots[1][0:2], places)
         before_2 = statistics_of_h(2)
         r_column(4)
         run(rows(2, False, False))
         weave(before_2[0:3], rows(3, False, False))
-        both_exponentials(0)
-        r_column(5)
+        exponentials(0)
+        exponentials(1)
         group_t(2, S.copy)
         group_t(3, S.copy)
-        run(before_2[3:] + maxima(1)[1:2] + maxima(2))
-        both_exponentials(1)
-        r_of(3)
-        run(maxima(3))
-        both_exponentials(2)
-        run(from_roots[2][0:2])
-        weave(rows(4, False, False), from_roots[2][2:])
-        run(rows(5, False, False) + rows(6, False, True))
+        r_column(5)
+        run(before_2[3:] + maxima(2))
+        exponentials(2)
+        exponentials(3)
+        r_column(6)
+        r_column(7)
+        run(rows(4, False, False))
+        weave(from_roots[2][0:2], rows(5, False, False))
+        exponentials(4)
         group_t(4, S.copy)
-        run(rows(7, False, True))
         group_t(5, S.copy)
+        run(rows(6, False, False) + rows(7, False, False))
         group_t(6, S.copy)
         quantise_t(0)
-        group_t(7, V.tensor_copy)
+        group_t(7, S.copy)
         second_contraction_pass(0)
-        exponentials(6)
-        r_of(4)
-        tanh_of_u(0)
+        exponentials(5)
+        maximum(6)
+        r_column(8)
         quantise_t(1)
         second_contraction_pass(1)
+        maximum(7)
+        tanh_of_u(0)
+        r_column(9)
         sums_of_v(0)
+        run(maxima(4))
+        exponentials(6)
+        tanh_of_u(1)
         exponentials(7)
         r_of(5)
-        run(maxima(4))
-        tanh_of_u(1)
         exponentials(8)
         steps, from_root = statistics_of_v(0, True)
         run(steps + maxima(5)[0:1])
         exponentials(9)
         sums_of_v(1)
         r_of(6)
-        run(maxima(5)[1:2])
         steps_1, from_root_1 = statistics_of_v(1, False)
         r_of(7)
-        weave(steps_1, maxima(6))
+        weave(steps_1, maxima(5)[1:2] + maxima(6)[0:1])
         both_exponentials(5)
-        run(maxima(7))
+        run(maxima(6)[1:2] + maxima(7))
         both_exponentials(6)
         both_exponentials(7)
         weight = weights_of_maxima()

@@ -25,6 +25,8 @@ ROUND = 4
 SETS = GROUPS * ROUND
 PAIR = 2
 EPS = 1e-5
+KEPT_BUSY_AT_Z = (4, 5, 6, 7)
+KEPT_BUSY_AT_T = (2, 4)
 OPERANDS = 4
 SPAN = QUAD * (P + WIDTH)
 
@@ -172,9 +174,17 @@ def tile_selfprojectiondev_pb_kernel(tc, x, o_xi, p_xi, rel_o_xi, out_0, out_1):
         h_inverses = {}
         h_shifts = {}
 
+        zeros = const.tile([P, P], BF16)
+        nc.vector.memset(zeros[:].bitcast(I32), 0)
+
+        def keep_busy(bank, moving):
+            nc.tensor.matmul(out=bank, lhsT=zeros[:], rhs=moving, start=True, stop=True)
+
         def first_pass(operand, b, tag):
             own = slice(operand * P, (operand + 1) * P)
             bank = psum_first.tile([P, LENGTH], F32, tag=tag, bufs=3 if tag == "r" else 2)
+            if tag == "z" and operand == 0 and b in KEPT_BUSY_AT_Z:
+                keep_busy(bank[:], x_groupeds[b][:, 0:P].rearrange("p c j -> p (c j)"))
             nc.tensor.matmul_mx(
                 out=bank[:],
                 lhsT=w_codes[:, own].bitcast(FP8X4),
@@ -326,6 +336,10 @@ def tile_selfprojectiondev_pb_kernel(tc, x, o_xi, p_xi, rel_o_xi, out_0, out_1):
                     scalar2=h_inverses[tile],
                     op0=ALU.subtract,
                     op1=ALU.mult,
+                )
+            if g == 0 and b in KEPT_BUSY_AT_T:
+                keep_busy(
+                    turned_t[b][:].rearrange("p u w -> p (u w)"), t_rows[:].rearrange("m u pj e -> m (u pj e)")
                 )
             words = t_rows[:].rearrange("m u pj e -> m (u pj e)").bitcast(F32)
             for u in range(2):
@@ -560,20 +574,20 @@ def tile_selfprojectiondev_pb_kernel(tc, x, o_xi, p_xi, rel_o_xi, out_0, out_1):
         weave(from_roots[1][0:2], places)
         before_2 = statistics_of_h(2)
         r_column(4)
-        run(rows(2, False, False))
-        weave(before_2[0:3], rows(3, False, False))
+        weave(rows(2, False, False), before_2[0:2])
+        r_column(5)
+        run(rows(3, False, False)[0:1] + before_2[2:3] + rows(3, False, False)[1:])
         exponentials(0)
         exponentials(1)
+        exponentials(2)
         group_t(2, S.copy)
         group_t(3, S.copy)
-        r_column(5)
         run(before_2[3:] + maxima(2))
-        exponentials(2)
         exponentials(3)
         r_column(6)
-        r_column(7)
         run(rows(4, False, False))
         weave(from_roots[2][0:2], rows(5, False, False))
+        r_column(7)
         exponentials(4)
         group_t(4, S.copy)
         group_t(5, S.copy)
@@ -585,11 +599,11 @@ def tile_selfprojectiondev_pb_kernel(tc, x, o_xi, p_xi, rel_o_xi, out_0, out_1):
         exponentials(5)
         maximum(6)
         r_column(8)
+        r_column(9)
         quantise_t(1)
         second_contraction_pass(1)
         maximum(7)
         tanh_of_u(0)
-        r_column(9)
         sums_of_v(0)
         run(maxima(4))
         exponentials(6)

@@ -25,8 +25,6 @@ ROUND = 4
 SETS = GROUPS * ROUND
 PAIR = 2
 EPS = 1e-5
-KEPT_BUSY_AT_Z = (4, 5, 6, 7)
-KEPT_BUSY_AT_T = (2, 4)
 OPERANDS = 4
 SPAN = QUAD * (P + WIDTH)
 
@@ -45,7 +43,6 @@ def statistics_steps(nc, pool, totals, sets, count, half):
     std = pool.tile([P, sets], F32, tag="std")
     std_eps = pool.tile([P, sets], F32, tag="std_eps")
     inverse = pool.tile([P, sets], F32, tag="inverse")
-    shift = pool.tile([P, sets], F32, tag="shift")
 
     def read_mean():
         nc.vector.tensor_copy(out=mean[:], in_=totals[:, 0:sets])
@@ -70,12 +67,7 @@ def statistics_steps(nc, pool, totals, sets, count, half):
     def invert():
         nc.vector.reciprocal(out=inverse[:], in_=std_eps[:])
 
-    def shift_step():
-        nc.vector.scalar_tensor_tensor(
-            out=shift[:], in0=mean[:], scalar=-1.0, in1=inverse[:], op0=ALU.mult, op1=ALU.mult
-        )
-
-    return mean, inverse, shift, [read_mean, square_mean, subtract, root], [add_eps, invert, shift_step]
+    return mean, inverse, [read_mean, square_mean, subtract, root], [add_eps, invert]
 
 
 def weave(small, large):
@@ -172,19 +164,10 @@ def tile_selfprojectiondev_pb_kernel(tc, x, o_xi, p_xi, rel_o_xi, out_0, out_1):
         h_tiles = []
         h_means = {}
         h_inverses = {}
-        h_shifts = {}
-
-        zeros = const.tile([P, P], BF16)
-        nc.vector.memset(zeros[:].bitcast(I32), 0)
-
-        def keep_busy(bank, moving):
-            nc.tensor.matmul(out=bank, lhsT=zeros[:], rhs=moving, start=True, stop=True)
 
         def first_pass(operand, b, tag):
             own = slice(operand * P, (operand + 1) * P)
             bank = psum_first.tile([P, LENGTH], F32, tag=tag, bufs=3 if tag == "r" else 2)
-            if tag == "z" and operand == 0 and b in KEPT_BUSY_AT_Z:
-                keep_busy(bank[:], x_groupeds[b][:, 0:P].rearrange("p c j -> p (c j)"))
             nc.tensor.matmul_mx(
                 out=bank[:],
                 lhsT=w_codes[:, own].bitcast(FP8X4),
@@ -251,14 +234,11 @@ def tile_selfprojectiondev_pb_kernel(tc, x, o_xi, p_xi, rel_o_xi, out_0, out_1):
             sets = GROUPS * items
             h_totals = psum_small.tile([P, 2 * sets], F32, tag="small")
             nc.tensor.matmul(out=h_totals[:], lhsT=quad_mean_h[:], rhs=h_stats[chain][:], start=True, stop=True)
-            h_mean, h_inverse, h_shift, to_root, from_root = statistics_steps(
-                nc, stats, h_totals, sets, LENGTH * WIDTH, half
-            )
+            h_mean, h_inverse, to_root, from_root = statistics_steps(nc, stats, h_totals, sets, LENGTH * WIDTH, half)
             from_roots[chain] = from_root
             for c in range(sets):
                 h_means[GROUPS * first + c] = h_mean[:, c : c + 1]
                 h_inverses[GROUPS * first + c] = h_inverse[:, c : c + 1]
-                h_shifts[GROUPS * first + c] = h_shift[:, c : c + 1]
             return to_root
 
         r_banks = {}
@@ -314,33 +294,20 @@ def tile_selfprojectiondev_pb_kernel(tc, x, o_xi, p_xi, rel_o_xi, out_0, out_1):
 
         turned_t = {}
 
-        def t_rows_of(b, g, on_scalar):
+        def t_rows_of(b, g):
             if g == 0:
                 transposed = psum_t.tile([P, 2, DEPTHS * WIDTH], F32)
                 turned_t[b] = transposed
             t_rows = t_work.tile([P, 2, P, 2], BF16)
             tile = GROUPS * b + g
-            if on_scalar:
-                nc.scalar.activation(
-                    out=t_rows[:],
-                    in_=h_tiles[tile][:],
-                    func=ACT.Identity,
-                    scale=h_inverses[tile],
-                    bias=h_shifts[tile],
-                )
-            else:
-                nc.vector.tensor_scalar(
-                    out=t_rows[:],
-                    in0=h_tiles[tile][:],
-                    scalar1=h_means[tile],
-                    scalar2=h_inverses[tile],
-                    op0=ALU.subtract,
-                    op1=ALU.mult,
-                )
-            if g == 0 and b in KEPT_BUSY_AT_T:
-                keep_busy(
-                    turned_t[b][:].rearrange("p u w -> p (u w)"), t_rows[:].rearrange("m u pj e -> m (u pj e)")
-                )
+            nc.vector.tensor_scalar(
+                out=t_rows[:],
+                in0=h_tiles[tile][:],
+                scalar1=h_means[tile],
+                scalar2=h_inverses[tile],
+                op0=ALU.subtract,
+                op1=ALU.mult,
+            )
             words = t_rows[:].rearrange("m u pj e -> m (u pj e)").bitcast(F32)
             for u in range(2):
                 nc.tensor.transpose(
@@ -409,9 +376,8 @@ def tile_selfprojectiondev_pb_kernel(tc, x, o_xi, p_xi, rel_o_xi, out_0, out_1):
             v_parts[rnd] = v_totals
 
         def statistics_of_v(rnd, on_scalar):
-            v_mean, v_inverse, v_shift, to_root, from_root = statistics_steps(
-                nc, stats, v_parts[rnd], SETS, WIDTH * WIDTH, half
-            )
+            v_totals = v_parts[rnd]
+            v_mean, v_inverse, to_root, from_root = statistics_steps(nc, stats, v_totals, SETS, WIDTH * WIDTH, half)
             centred = per_round.tile([P, SETS, WIDTH], F32)
             proj = per_round.tile([P, SETS, WIDTH], F32)
 
@@ -423,38 +389,49 @@ def tile_selfprojectiondev_pb_kernel(tc, x, o_xi, p_xi, rel_o_xi, out_0, out_1):
                     op=ALU.subtract,
                 )
 
-            def scale():
-                nc.vector.tensor_tensor(
-                    out=proj[:],
-                    in0=centred[:],
-                    in1=v_inverse[:].unsqueeze(2).to_broadcast([P, SETS, WIDTH]),
-                    op=ALU.mult,
+            def store(g):
+                nc.sync.dma_start(
+                    out=out_0[rnd * ROUND : (rnd + 1) * ROUND, g * QUAD : (g + 1) * QUAD].rearrange(
+                        "b d p w -> (d p) b w"
+                    ),
+                    in_=proj[:, g * ROUND : (g + 1) * ROUND, :],
                 )
-                store()
 
-            def store():
+            def scale():
                 for g in range(GROUPS):
-                    nc.sync.dma_start(
-                        out=out_0[rnd * ROUND : (rnd + 1) * ROUND, g * QUAD : (g + 1) * QUAD].rearrange(
-                            "b d p w -> (d p) b w"
-                        ),
-                        in_=proj[:, g * ROUND : (g + 1) * ROUND, :],
+                    own = slice(g * ROUND, (g + 1) * ROUND)
+                    nc.vector.tensor_tensor(
+                        out=proj[:, own, :],
+                        in0=centred[:, own, :],
+                        in1=v_inverse[:, own].unsqueeze(2).to_broadcast([P, ROUND, WIDTH]),
+                        op=ALU.mult,
                     )
+                    store(g)
 
-            def standardise_on_scalar():
+            neg_mean = stats.tile([P, SETS], F32)
+
+            def negate_mean():
+                nc.vector.tensor_scalar(
+                    out=neg_mean[:], in0=v_totals[:, 0:SETS], scalar1=-1.0, scalar2=None, op0=ALU.mult
+                )
+
+            def centre_on_scalar():
                 for s in range(SETS):
                     nc.scalar.activation(
-                        out=proj[:, s, :],
-                        in_=v_tiles[rnd][:, s, :],
-                        func=ACT.Identity,
-                        scale=v_inverse[:, s : s + 1],
-                        bias=v_shift[:, s : s + 1],
+                        out=centred[:, s, :], in_=v_tiles[rnd][:, s, :], func=ACT.Identity, bias=neg_mean[:, s : s + 1]
                     )
-                store()
+
+            def scale_on_scalar():
+                for s in range(SETS):
+                    nc.scalar.activation(
+                        out=proj[:, s, :], in_=centred[:, s, :], func=ACT.Copy, scale=v_inverse[:, s : s + 1]
+                    )
+                for g in range(GROUPS):
+                    store(g)
 
             if on_scalar:
-                return to_root, from_root + [standardise_on_scalar]
-            return to_root, [from_root[0], centre, from_root[1], scale]
+                return to_root[0:2] + [negate_mean] + to_root[2:], from_root + [centre_on_scalar, scale_on_scalar]
+            return to_root, from_root + [centre, scale]
 
         shape = [BATCH * GROUPS, QUAD, WIDTH]
 
@@ -463,19 +440,25 @@ def tile_selfprojectiondev_pb_kernel(tc, x, o_xi, p_xi, rel_o_xi, out_0, out_1):
             nc.tensor.transpose(out=turned_tile[:], in_=statistic[:], identity=ident_f[:])
             return turned_tile[0 : BATCH * GROUPS, :].rearrange("r (d w) -> r d w", w=WIDTH)
 
-        def weights_of_maxima():
+        weight = const.tile(shape, F32)
+
+        def weight_steps():
             neg_max_t = turned(neg_max)
             neg_top = const.tile(shape[0:2], F32)
-            nc.vector.tensor_reduce(out=neg_top[:], in_=neg_max_t, axis=AXIS.X, op=ALU.min)
             below_top = const.tile(shape, F32)
-            nc.vector.tensor_tensor(
-                out=below_top[:], in0=neg_top[:].unsqueeze(2).to_broadcast(shape), in1=neg_max_t, op=ALU.subtract
-            )
-            weight = const.tile(shape, F32)
-            nc.scalar.activation(out=weight[:], in_=below_top[:], func=ACT.Exp)
-            return weight
 
-        def mass_steps(weight):
+            def find_top():
+                nc.vector.tensor_reduce(out=neg_top[:], in_=neg_max_t, axis=AXIS.X, op=ALU.min)
+
+            def measure():
+                nc.vector.tensor_tensor(
+                    out=below_top[:], in0=neg_top[:].unsqueeze(2).to_broadcast(shape), in1=neg_max_t, op=ALU.subtract
+                )
+                nc.scalar.activation(out=weight[:], in_=below_top[:], func=ACT.Exp)
+
+            return [find_top, measure]
+
+        def mass_steps():
             exp_sum_t = turned(exp_sum)
             share = const.tile(shape, F32)
             whole = const.tile(shape[0:2], F32)
@@ -504,8 +487,8 @@ def tile_selfprojectiondev_pb_kernel(tc, x, o_xi, p_xi, rel_o_xi, out_0, out_1):
         def later(function, *arguments):
             return lambda: function(*arguments)
 
-        def rows(b, *on_scalar):
-            return [later(t_rows_of, b, g, on_scalar[g]) for g in range(GROUPS)]
+        def rows(b):
+            return [later(t_rows_of, b, g) for g in range(GROUPS)]
 
         def maxima(*items):
             return [later(maximum, GROUPS * b + g) for b in items for g in range(GROUPS)]
@@ -559,12 +542,12 @@ def tile_selfprojectiondev_pb_kernel(tc, x, o_xi, p_xi, rel_o_xi, out_0, out_1):
         weave(from_roots[0][0:2], [later(quantise_x, 6)])
         tanh_of_z(6)
         before_1 = statistics_of_h(1)
-        run(rows(0, False, False)[0:1])
+        run(rows(0)[0:1])
         regroup_x(7)
-        run(rows(0, False, False)[1:])
+        run(rows(0)[1:])
         quantise_x(7)
         tanh_of_z(7)
-        weave(before_1, rows(1, False, False))
+        weave(before_1, rows(1))
         r_column(2)
         group_t(0, V.tensor_copy)
         group_t(1, V.tensor_copy)
@@ -574,9 +557,9 @@ def tile_selfprojectiondev_pb_kernel(tc, x, o_xi, p_xi, rel_o_xi, out_0, out_1):
         weave(from_roots[1][0:2], places)
         before_2 = statistics_of_h(2)
         r_column(4)
-        weave(rows(2, False, False), before_2[0:2])
+        weave(rows(2), before_2[0:2])
         r_column(5)
-        run(rows(3, False, False)[0:1] + before_2[2:3] + rows(3, False, False)[1:])
+        run(rows(3)[0:1] + before_2[2:3] + rows(3)[1:])
         exponentials(0)
         exponentials(1)
         exponentials(2)
@@ -585,13 +568,13 @@ def tile_selfprojectiondev_pb_kernel(tc, x, o_xi, p_xi, rel_o_xi, out_0, out_1):
         run(before_2[3:] + maxima(2))
         exponentials(3)
         r_column(6)
-        run(rows(4, False, False))
-        weave(from_roots[2][0:2], rows(5, False, False))
+        run(rows(4))
+        weave(from_roots[2][0:2], rows(5))
         r_column(7)
         exponentials(4)
         group_t(4, S.copy)
         group_t(5, S.copy)
-        run(rows(6, False, False) + rows(7, False, False))
+        run(rows(6) + rows(7))
         group_t(6, S.copy)
         quantise_t(0)
         group_t(7, S.copy)
@@ -613,16 +596,19 @@ def tile_selfprojectiondev_pb_kernel(tc, x, o_xi, p_xi, rel_o_xi, out_0, out_1):
         exponentials(8)
         steps, from_root = statistics_of_v(0, True)
         run(steps + maxima(5)[0:1])
+        from_root[2]()
         exponentials(9)
         sums_of_v(1)
         r_of(6)
         steps_1, from_root_1 = statistics_of_v(1, False)
         r_of(7)
-        weave(steps_1, maxima(5)[1:2] + maxima(6)[0:1])
+        weave(steps_1[0:3], maxima(5)[1:2] + maxima(6)[0:1])
+        run(from_root[0:1] + steps_1[3:] + from_root[1:2])
         both_exponentials(5)
+        from_root[3]()
         run(maxima(6)[1:2] + maxima(7))
         both_exponentials(6)
         both_exponentials(7)
-        weight = weights_of_maxima()
-        run(from_root[0:1] + from_root_1[0:1] + from_root[1:2] + from_root_1[1:2] + from_root[2:])
-        weave(mass_steps(weight), from_root_1[2:])
+        weights = weight_steps()
+        run(weights[0:1] + from_root_1[0:1] + from_root_1[2:3] + from_root_1[1:2] + weights[1:])
+        run(from_root_1[3:] + mass_steps())

from contextlib import ExitStack

import concourse.mybir as mybir
from concourse.masks import make_identity

BF16 = mybir.dt.bfloat16
F32 = mybir.dt.float32
I32 = mybir.dt.int32
U32 = mybir.dt.uint32
U8 = mybir.dt.uint8
FP8X4 = mybir.dt.float8_e4m3fn_x4
ACT = mybir.ActivationFunctionType
ALU = mybir.AluOpType
AXIS = mybir.AxisListType

P = 128
PACK = 4
BATCH = 8
LENGTH = 512
WIDTH = 32
DEPTHS = 8
QUAD = P // WIDTH
GROUPS = DEPTHS // QUAD
ROUND = 4
SETS = GROUPS * ROUND
PAIR = 2
EPS = 1e-5
OPERANDS = 4
SPAN = QUAD * (P + WIDTH)

FLOPS = 2 * BATCH * DEPTHS * (2 * LENGTH * LENGTH * WIDTH + LENGTH * WIDTH * WIDTH)


def quantise(nc, codes, scales, grouped):
    nc.vector.quantize_mx(out=codes.bitcast(FP8X4), scales=scales, in_=grouped)


def statistics_steps(nc, pool, totals, sets, count, half):
    mean = pool.tile([P, sets], F32, tag="mean")
    mean_squared = pool.tile([P, sets], F32, tag="mean_squared")
    spread = pool.tile([P, sets], F32, tag="spread")
    variance = pool.tile([P, sets], F32, tag="variance")
    std = pool.tile([P, sets], F32, tag="std")
    std_eps = pool.tile([P, sets], F32, tag="std_eps")
    inverse = pool.tile([P, sets], F32, tag="inverse")

    def read_mean():
        nc.vector.tensor_copy(out=mean[:], in_=totals[:, 0:sets])

    def square_mean():
        nc.vector.tensor_tensor(out=mean_squared[:], in0=totals[:, 0:sets], in1=mean[:], op=ALU.mult)

    def subtract():
        nc.vector.tensor_tensor(
            out=spread[:], in0=totals[:, sets : 2 * sets], in1=mean_squared[:], op=ALU.subtract
        )

    def root():
        nc.vector.tensor_scalar(
            out=variance[:], in0=spread[:], scalar1=count / (count - 1), scalar2=0.0, op0=ALU.mult, op1=ALU.max
        )
        nc.gpsimd.tensor_tensor(out=std[:], in0=variance[:], in1=half[:, 0:sets], op=ALU.pow)

    def add_eps():
        nc.vector.tensor_scalar_add(out=std_eps[:], in0=std[:], scalar1=EPS)

    def invert():
        nc.vector.reciprocal(out=inverse[:], in_=std_eps[:])

    return mean, inverse, [read_mean, square_mean, subtract, root], [add_eps, invert]


def weave(small, large):
    for i in range(max(len(small), len(large))):
        if i < len(small):
            small[i]()
        if i < len(large):
            large[i]()


def tile_selfprojectiondev_pb_kernel(tc, x, o_xi, p_xi, rel_o_xi, out_0, out_1):
    nc = tc.nc
    with ExitStack() as stack:
        const = stack.enter_context(tc.tile_pool(name="const", bufs=1))
        x_in = stack.enter_context(tc.tile_pool(name="x_in", bufs=BATCH))
        x_work = stack.enter_context(tc.tile_pool(name="x_work", bufs=3))
        x_keep = stack.enter_context(tc.tile_pool(name="x_keep", bufs=BATCH))
        h_pool = stack.enter_context(tc.tile_pool(name="h_pool", bufs=GROUPS * BATCH))
        unread = stack.enter_context(tc.tile_pool(name="unread", bufs=4))
        t_work = stack.enter_context(tc.tile_pool(name="t_work", bufs=2 * ROUND))
        per_round = stack.enter_context(tc.tile_pool(name="per_round", bufs=2))
        stats = stack.enter_context(tc.tile_pool(name="stats", bufs=6))
        psum_first = stack.enter_context(tc.psum_pool(name="psum_first", bufs=2))
        psum_t = stack.enter_context(tc.psum_pool(name="psum_t", bufs=2))
        psum_small = stack.enter_context(tc.psum_pool(name="psum_small", bufs=1))

        w_raw = const.tile([P, OPERANDS, QUAD, PACK * WIDTH], BF16)
        p_raw = const.tile([P, DEPTHS, PACK * WIDTH], BF16)
        x_raws = []

        def load_x(b, rows=slice(0, PACK)):
            if b == len(x_raws):
                x_raw = x_in.tile([P, PACK, LENGTH], BF16)
                x_raws.append(x_raw)
            nc.sync.dma_start(out=x_raws[b][:, rows], in_=x[b].rearrange("(p j) c -> p j c", j=PACK)[:, rows])

        def load_w(n):
            source = o_xi if n < GROUPS else rel_o_xi
            g = n % GROUPS
            nc.sync.dma_start(
                out=w_raw[:, n], in_=source[g * QUAD : (g + 1) * QUAD].rearrange("d (p j) w -> p d (j w)", j=PACK)
            )

        load_x(0, slice(0, 2))
        load_x(0, slice(2, PACK))
        load_w(0)
        load_w(1)
        load_x(1)
        load_w(2)
        load_w(3)
        load_x(2)
        load_x(3)
        nc.sync.dma_start(out=p_raw[:], in_=p_xi.rearrange("d (p j) w -> p d (j w)", j=PACK))
        for b in range(4, BATCH):
            load_x(b)

        half = const.tile([P, SETS], F32)
        nc.gpsimd.memset(half[:], 0.5)
        warm = const.tile([P, 1], F32)
        nc.scalar.activation(out=warm[:], in_=half[:, 0:1], func=ACT.Tanh)
        ident_f = const.tile([P, P], F32)
        make_identity(nc, ident_f[:])
        quad_mean_h = const.tile([P, P], F32)
        quad_mean_v = const.tile([P, P], F32)
        for quad_mean, count in ((quad_mean_h, LENGTH * WIDTH), (quad_mean_v, WIDTH * WIDTH)):
            nc.vector.memset(quad_mean[:], 0.0)
            for q in range(QUAD):
                rows = slice(q * WIDTH, (q + 1) * WIDTH)
                nc.vector.memset(quad_mean[rows, rows], 1.0 / count)
        neg_max = const.tile([P, P], F32)
        nc.vector.memset(neg_max[:], 0.0)
        exp_sum = const.tile([P, P], F32)
        nc.vector.memset(exp_sum[:], 0.0)

        w_grouped = const.tile([P, OPERANDS, P, PACK], BF16, align_bytes=64)
        w_codes = const.tile([P, OPERANDS * P], U32, align_bytes=64)
        w_scales = const.tile([P, OPERANDS * P], U8, align_bytes=64)

        def regroup_w(n, copy):
            copy(
                out=w_grouped[:, n].rearrange("p (d w) j -> p d w j", w=WIDTH),
                in_=w_raw[:, n].rearrange("p d (j w) -> p d w j", j=PACK),
            )

        def quantise_w(first, last):
            own = slice(first * P, (last + 1) * P)
            quantise(
                nc, w_codes[:, own], w_scales[:, own], w_grouped[:, first : last + 1].rearrange("p n c j -> p (n c j)")
            )

        x_groupeds = []
        x_codes = []
        x_scales = []
        h_tiles = []
        h_means = {}
        h_inverses = {}

        def first_pass(operand, b, tag):
            own = slice(operand * P, (operand + 1) * P)
            bank = psum_first.tile([P, LENGTH], F32, tag=tag, bufs=3 if tag == "r" else 2)
            nc.tensor.matmul_mx(
                out=bank[:],
                lhsT=w_codes[:, own].bitcast(FP8X4),
                lhsT_scale=w_scales[:, own],
                rhs=x_codes[b][:].bitcast(FP8X4),
                rhs_scale=x_scales[b][:],
                start=True,
                stop=True,
            )
            return bank

        def regroup_x(b, rows=slice(0, PACK)):
            if b == len(x_groupeds):
                x_grouped = x_work.tile([P, LENGTH, PACK], BF16, align_bytes=64)
                x_groupeds.append(x_grouped)
            nc.vector.tensor_copy(
                out=x_groupeds[b][:, :, rows].rearrange("p (c i) j -> p c j i", i=4),
                in_=x_raws[b][:, rows].rearrange("p j (c i) -> p c j i", i=4),
            )

        def quantise_x(b):
            codes = x_keep.tile([P, LENGTH], U32, align_bytes=64)
            scales = x_keep.tile([P, LENGTH], U8, align_bytes=64)
            x_codes.append(codes)
            x_scales.append(scales)
            quantise(nc, codes[:], scales[:], x_groupeds[b][:].rearrange("p c j -> p (c j)"))

        h_stats = []
        CHAINS = ((0, 2), (2, 4), (6, 2))
        chain_of = {}
        for first, items in CHAINS:
            h_stat = stats.tile([P, 2 * GROUPS * items], F32)
            h_stats.append(h_stat)
            for b in range(first, first + items):
                chain_of[b] = (h_stat, first, items)

        def tanh_of_z(b):
            h_stat, first, items = chain_of[b]
            for g in range(GROUPS):
                col = GROUPS * (b - first) + g
                z_bank = first_pass(g, b, "z")
                h = h_pool.tile([P, 2, P, 2], F32)
                nc.scalar.activation(
                    out=h[:],
                    in_=z_bank[:].rearrange("m (pj u e) -> m u pj e", u=2, e=2),
                    func=ACT.Tanh,
                    accum_out=h_stat[:, col : col + 1],
                )
                h_tiles.append(h)
            for g in range(GROUPS):
                col = GROUPS * (items + b - first) + g
                h_squared = unread.tile([P, 2, P, 2], BF16, tag="unread")
                nc.scalar.activation(
                    out=h_squared[:],
                    in_=h_tiles[GROUPS * b + g][:],
                    func=ACT.Square,
                    accum_out=h_stat[:, col : col + 1],
                )

        from_roots = {}

        def statistics_of_h(chain):
            first, items = CHAINS[chain]
            sets = GROUPS * items
            h_totals = psum_small.tile([P, 2 * sets], F32, tag="small")
            nc.tensor.matmul(out=h_totals[:], lhsT=quad_mean_h[:], rhs=h_stats[chain][:], start=True, stop=True)
            h_mean, h_inverse, to_root, from_root = statistics_steps(nc, stats, h_totals, sets, LENGTH * WIDTH, half)
            from_roots[chain] = from_root
            for c in range(sets):
                h_means[GROUPS * first + c] = h_mean[:, c : c + 1]
                h_inverses[GROUPS * first + c] = h_inverse[:, c : c + 1]
            return to_root

        r_banks = {}

        def r_of(b):
            for g in range(GROUPS):
                r_column(GROUPS * b + g)

        def r_column(col):
            r_bank = first_pass(GROUPS + col % GROUPS, col // GROUPS, "r" if col % 5 < 3 else "z")
            r_banks[col] = r_bank

        def maximum(col):
            nc.vector.tensor_reduce(
                out=neg_max[:, col : col + 1], in_=r_banks[col][:], axis=AXIS.X, op=ALU.max, negate=True
            )

        def exponentials(col):
            exp_r = unread.tile([P, LENGTH], BF16, tag="unread")
            nc.scalar.activation(
                out=exp_r[:],
                in_=r_banks[col][:],
                func=ACT.Exp,
                bias=neg_max[:, col : col + 1],
                accum_out=exp_sum[:, col : col + 1],
            )

        p_grouped = const.tile([P, DEPTHS * WIDTH, PACK], BF16, align_bytes=64)
        p_codes = const.tile([P, DEPTHS * WIDTH], U32, align_bytes=64)
        p_scales = const.tile([P, DEPTHS * WIDTH], U8, align_bytes=64)
        pz_codes = const.tile([P, GROUPS * SPAN], U32, align_bytes=64)
        pz_scales = const.tile([P, GROUPS * SPAN], U8, align_bytes=64)
        nc.vector.memset(pz_codes[:].bitcast(I32), 0)
        nc.vector.memset(pz_scales[:].bitcast(I32), 0)
        nc.vector.memset(p_scales[:].bitcast(I32), 0)

        def regroup_p():
            nc.vector.tensor_copy(
                out=p_grouped[:].rearrange("p (d w) j -> p d w j", w=WIDTH),
                in_=p_raw[:].rearrange("p d (j w) -> p d w j", j=PACK),
            )

        def quantise_p():
            quantise(nc, p_codes[:], p_scales[:], p_grouped[:].rearrange("p c j -> p (c j)"))

        def place_p(source, target):
            nc.vector.tensor_copy(
                out=target.rearrange("p (d s) -> p d s", s=P + WIDTH)[:, :, 0:WIDTH],
                in_=source.rearrange("p (d w) -> p d w", w=WIDTH),
            )

        t_groupeds = {}

        turned_t = {}

        def t_rows_of(b, g):
            if g == 0:
                transposed = psum_t.tile([P, 2, DEPTHS * WIDTH], F32)
                turned_t[b] = transposed
            t_rows = t_work.tile([P, 2, P, 2], BF16)
            tile = GROUPS * b + g
            nc.vector.tensor_scalar(
                out=t_rows[:],
                in0=h_tiles[tile][:],
                scalar1=h_means[tile],
                scalar2=h_inverses[tile],
                op0=ALU.subtract,
                op1=ALU.mult,
            )
            words = t_rows[:].rearrange("m u pj e -> m (u pj e)").bitcast(F32)
            for u in range(2):
                nc.tensor.transpose(
                    out=turned_t[b][:, u, g * P : (g + 1) * P], in_=words[:, u * P : (u + 1) * P], identity=ident_f[:]
                )

        def group_t(b, copy):
            rnd, bi = divmod(b, ROUND)
            if rnd not in t_groupeds:
                t_grouped = per_round.tile([P, DEPTHS * ROUND * WIDTH * PACK], BF16, align_bytes=64)
                t_groupeds[rnd] = t_grouped
            words = t_groupeds[rnd][:].bitcast(F32).rearrange("p (d b w u) -> p d b w u", b=ROUND, w=WIDTH, u=2)
            copy(out=words[:, :, bi], in_=turned_t[b][:].rearrange("p u (d w) -> p d w u", w=WIDTH))

        v_tiles = {}
        v_stats = {}
        t_operands = {}

        def quantise_t(rnd):
            t_codes = per_round.tile([P, DEPTHS * P], U32, align_bytes=64)
            t_scales = per_round.tile([P, DEPTHS * P], U8, align_bytes=64)
            quantise(nc, t_codes[:], t_scales[:], t_groupeds[rnd][:])
            t_operands[rnd] = (t_codes, t_scales)

        u_banks = {}

        def second_contraction_pass(rnd):
            t_codes, t_scales = t_operands[rnd]
            u_bank = psum_small.tile([P, GROUPS, ROUND * WIDTH], F32, tag="small")
            for g in range(GROUPS):
                for q in range(QUAD):
                    own = slice((g * QUAD + q) * P, (g * QUAD + q + 1) * P)
                    padded = slice(g * SPAN + q * P, g * SPAN + (q + 1) * P)
                    nc.tensor.matmul_mx(
                        out=u_bank[:, g, :],
                        lhsT=pz_codes[:, padded].bitcast(FP8X4),
                        lhsT_scale=pz_scales[:, padded],
                        rhs=t_codes[:, own].bitcast(FP8X4),
                        rhs_scale=t_scales[:, own],
                        start=(q == 0),
                        stop=(q == QUAD - 1),
                    )
            u_banks[rnd] = u_bank

        def tanh_of_u(rnd):
            v = per_round.tile([P, SETS, WIDTH], F32)
            v_stat = per_round.tile([P, 2 * SETS], F32)
            u = u_banks[rnd][:].rearrange("m g (b w) -> m (g b) w", w=WIDTH)
            for s in range(SETS):
                nc.scalar.activation(
                    out=v[:, s, :], in_=u[:, s, :], func=ACT.Tanh, accum_out=v_stat[:, s : s + 1]
                )
            for s in range(SETS):
                v_squared = unread.tile([P, WIDTH], BF16, tag="unread_v")
                nc.scalar.activation(
                    out=v_squared[:], in_=v[:, s, :], func=ACT.Square, accum_out=v_stat[:, SETS + s : SETS + s + 1]
                )
            v_tiles[rnd] = v
            v_stats[rnd] = v_stat

        v_parts = {}

        def sums_of_v(rnd):
            v_totals = psum_small.tile([P, 2 * SETS], F32, tag="small")
            nc.tensor.matmul(out=v_totals[:], lhsT=quad_mean_v[:], rhs=v_stats[rnd][:], start=True, stop=True)
            v_parts[rnd] = v_totals

        def statistics_of_v(rnd, on_scalar):
            v_totals = v_parts[rnd]
            v_mean, v_inverse, to_root, from_root = statistics_steps(nc, stats, v_totals, SETS, WIDTH * WIDTH, half)
            centred = per_round.tile([P, SETS, WIDTH], F32)
            proj = per_round.tile([P, SETS, WIDTH], F32)

            def centre():
                nc.vector.tensor_tensor(
                    out=centred[:],
                    in0=v_tiles[rnd][:],
                    in1=v_mean[:].unsqueeze(2).to_broadcast([P, SETS, WIDTH]),
                    op=ALU.subtract,
                )

            def store(g):
                nc.sync.dma_start(
                    out=out_0[rnd * ROUND : (rnd + 1) * ROUND, g * QUAD : (g + 1) * QUAD].rearrange(
                        "b d p w -> (d p) b w"
                    ),
                    in_=proj[:, g * ROUND : (g + 1) * ROUND, :],
                )

            def scale():
                for g in range(GROUPS):
                    own = slice(g * ROUND, (g + 1) * ROUND)
                    nc.vector.tensor_tensor(
                        out=proj[:, own, :],
                        in0=centred[:, own, :],
                        in1=v_inverse[:, own].unsqueeze(2).to_broadcast([P, ROUND, WIDTH]),
                        op=ALU.mult,
                    )
                    store(g)

            neg_mean = stats.tile([P, SETS], F32)

            def negate_mean():
                nc.vector.tensor_scalar(
                    out=neg_mean[:], in0=v_totals[:, 0:SETS], scalar1=-1.0, scalar2=None, op0=ALU.mult
                )

            def centre_on_scalar():
                for s in range(SETS):
                    nc.scalar.activation(
                        out=centred[:, s, :], in_=v_tiles[rnd][:, s, :], func=ACT.Identity, bias=neg_mean[:, s : s + 1]
                    )

            def scale_on_scalar():
                for s in range(SETS):
                    nc.scalar.activation(
                        out=proj[:, s, :], in_=centred[:, s, :], func=ACT.Copy, scale=v_inverse[:, s : s + 1]
                    )
                for g in range(GROUPS):
                    store(g)

            if on_scalar:
                return to_root[0:2] + [negate_mean] + to_root[2:], from_root + [centre_on_scalar, scale_on_scalar]
            return to_root, from_root + [centre, scale]

        shape = [BATCH * GROUPS, QUAD, WIDTH]

        def turned(statistic):
            turned_tile = psum_t.tile([P, P], F32, tag="transposed")
            nc.tensor.transpose(out=turned_tile[:], in_=statistic[:], identity=ident_f[:])
            return turned_tile[0 : BATCH * GROUPS, :].rearrange("r (d w) -> r d w", w=WIDTH)

        weight = const.tile(shape, F32)

        def weight_steps():
            neg_max_t = turned(neg_max)
            neg_top = const.tile(shape[0:2], F32)
            below_top = const.tile(shape, F32)

            def find_top():
                nc.vector.tensor_reduce(out=neg_top[:], in_=neg_max_t, axis=AXIS.X, op=ALU.min)

            def measure():
                nc.vector.tensor_tensor(
                    out=below_top[:], in0=neg_top[:].unsqueeze(2).to_broadcast(shape), in1=neg_max_t, op=ALU.subtract
                )
                nc.scalar.activation(out=weight[:], in_=below_top[:], func=ACT.Exp)

            return [find_top, measure]

        def mass_steps():
            exp_sum_t = turned(exp_sum)
            share = const.tile(shape, F32)
            whole = const.tile(shape[0:2], F32)
            whole_inverse = const.tile(shape[0:2], F32)
            mass = const.tile(shape, F32)

            def weigh():
                nc.vector.tensor_tensor(out=share[:], in0=weight[:], in1=exp_sum_t, op=ALU.mult)

            def add_up():
                nc.vector.tensor_reduce(out=whole[:], in_=share[:], axis=AXIS.X, op=ALU.add)

            def invert_whole():
                nc.vector.reciprocal(out=whole_inverse[:], in_=whole[:])

            def store():
                nc.vector.tensor_tensor(
                    out=mass[:], in0=share[:], in1=whole_inverse[:].unsqueeze(2).to_broadcast(shape), op=ALU.mult
                )
                nc.sync.dma_start(out=out_1.rearrange("b (g d) w -> (b g) d w", g=GROUPS), in_=mass[:])

            return [weigh, add_up, invert_whole, store]

        V, S = nc.vector, nc.scalar

        def later(function, *arguments):
            return lambda: function(*arguments)

        def rows(b):
            return [later(t_rows_of, b, g) for g in range(GROUPS)]

        def maxima(*items):
            return [later(maximum, GROUPS * b + g) for b in items for g in range(GROUPS)]

        def run(steps):
            for step in steps:
                step()

        def both_exponentials(b):
            for g in range(GROUPS):
                exponentials(GROUPS * b + g)

        places = [
            later(place_p, p_codes[:].bitcast(I32), pz_codes[:].bitcast(I32)),
            later(place_p, p_scales[:], pz_scales[:]),
        ]

        stack.enter_context(tc.manual_schedule())
        regroup_x(0, slice(0, 2))
        regroup_x(0, slice(2, PACK))
        regroup_w(0, S.copy)
        regroup_w(1, S.copy)
        quantise_x(0)
        quantise_w(0, 0)
        quantise_w(1, 1)
        tanh_of_z(0)
        regroup_x(1)
        regroup_w(2, V.tensor_copy)
        quantise_x(1)
        tanh_of_z(1)
        regroup_w(3, V.tensor_copy)
        regroup_x(2)
        quantise_w(2, 3)
        quantise_x(2)
        tanh_of_z(2)
        before_0 = statistics_of_h(0)
        r_of(0)
        regroup_x(3)
        regroup_p()
        quantise_x(3)
        tanh_of_z(3)
        quantise_p()
        regroup_x(4)
        weave(before_0[0:2], [later(quantise_x, 4), later(regroup_x, 5)])
        tanh_of_z(4)
        run(before_0[2:3])
        quantise_x(5)
        tanh_of_z(5)
        run(before_0[3:] + maxima(0))
        regroup_x(6)
        weave(from_roots[0][0:2], [later(quantise_x, 6)])
        tanh_of_z(6)
        before_1 = statistics_of_h(1)
        run(rows(0)[0:1])
        regroup_x(7)
        run(rows(0)[1:])
        quantise_x(7)
        tanh_of_z(7)
        weave(before_1, rows(1))
        r_column(2)
        group_t(0, V.tensor_copy)
        group_t(1, V.tensor_copy)
        maximum(2)
        r_column(3)
        maximum(3)
        weave(from_roots[1][0:2], places)
        before_2 = statistics_of_h(2)
        r_column(4)
        weave(rows(2), before_2[0:2])
        r_column(5)
        run(rows(3)[0:1] + before_2[2:3] + rows(3)[1:])
        exponentials(0)
        exponentials(1)
        exponentials(2)
        group_t(2, S.copy)
        group_t(3, S.copy)
        run(before_2[3:] + maxima(2))
        exponentials(3)
        r_column(6)
        run(rows(4))
        weave(from_roots[2][0:2], rows(5))
        r_column(7)
        exponentials(4)
        group_t(4, S.copy)
        group_t(5, S.copy)
        run(rows(6) + rows(7))
        group_t(6, S.copy)
        quantise_t(0)
        group_t(7, S.copy)
        second_contraction_pass(0)
        exponentials(5)
        maximum(6)
        r_column(8)
        r_column(9)
        quantise_t(1)
        second_contraction_pass(1)
        maximum(7)
        tanh_of_u(0)
        sums_of_v(0)
        run(maxima(4))
        exponentials(6)
        tanh_of_u(1)
        exponentials(7)
        r_of(5)
        exponentials(8)
        steps, from_root = statistics_of_v(0, True)
        run(steps + maxima(5)[0:1])
        from_root[2]()
        exponentials(9)
        sums_of_v(1)
        r_of(6)
        steps_1, from_root_1 = statistics_of_v(1, False)
        r_of(7)
        weave(steps_1[0:3], maxima(5)[1:2] + maxima(6)[0:1])
        run(from_root[0:1] + steps_1[3:] + from_root[1:2])
        both_exponentials(5)
        from_root[3]()
        run(maxima(6)[1:2] + maxima(7))
        both_exponentials(6)
        both_exponentials(7)
        weights = weight_steps()
        run(weights[0:1] + from_root_1[0:1] + from_root_1[2:3] + from_root_1[1:2] + weights[1:])
        run(from_root_1[3:] + mass_steps())
